import numpy as np
import ml_dtypes


def mxq(x, axis, fmt="e4m3"):
    dtype, down = {"e4m3": (ml_dtypes.float8_e4m3fn, 7), "e5m2": (ml_dtypes.float8_e5m2, 14)}[fmt]
    v = np.moveaxis(np.asarray(x, np.float32).astype(ml_dtypes.bfloat16).astype(np.float64), axis, -1)
    blocks = v.reshape(v.shape[:-1] + (-1, 32))
    amax = np.abs(blocks).max(-1, keepdims=True)
    byte = np.maximum(np.where(amax > 0, np.frexp(amax)[1] - 1 + 127, 0) - down, 1)
    scale = np.exp2(byte - 127.0)
    codes = (blocks / scale).astype(np.float32).astype(dtype).astype(np.float64)
    return np.moveaxis((codes * scale).reshape(v.shape), -1, axis)


WIDE = False


def mx_kscale(k):
    if not WIDE:
        return np.ones(k)
    levels = np.array([10, -10, 5, -5, 0])
    a = np.random.permutation(np.resize(levels, k // 512 * 4)).reshape(k // 512, 4)
    idx = np.arange(k)
    return np.exp2(a[idx // 512, idx % 128 // 32])


BF16 = ml_dtypes.bfloat16


def bf(x):
    return np.asarray(x, np.float32).astype(BF16)


def f64(x):
    return np.asarray(x).astype(np.float64)


K = 3
PAD = (K - 1) // 2
UM = 2
C_IN = 512
C_OUT = 512
SLOPE = 0.01
NB, HH, WW = 2, 32, 32


def setup_inputs():
    s = mx_kscale(C_IN)
    f = np.array([1.0, s.min() / s.max()])
    noise = np.random.standard_normal((NB, C_IN // UM, UM, HH, WW))
    level = np.random.standard_normal((NB, 1, UM, 1, 1)) + 0.5 * np.random.standard_normal((NB, 1, UM, HH, WW))
    fc = np.tile(f, C_IN // UM)
    return {"xx": bf(((noise + level) * f.reshape(1, 1, UM, 1, 1)).reshape(NB, C_IN, HH, WW)),
            "w": bf(np.random.standard_normal((C_OUT, C_IN, K, K)) * 0.0147 / fc[None, :, None, None]),
            "b": bf(np.random.standard_normal(C_OUT) * 0.3)}


def reference(xx, w, b):
    xx, w, b = f64(xx), f64(w), f64(b)
    B, C, H, Wd = xx.shape
    xp = np.pad(xx, ((0, 0), (0, 0), (PAD, PAD), (PAD, PAD)), mode="edge")
    patches = np.stack(
        [np.stack([xp[:, :, r:r + H, s:s + Wd] for s in range(K)], axis=2)
         for r in range(K)], axis=2)
    g = patches.reshape(B, C // UM, UM, K, K, H, Wd)
    avgs = g.mean(axis=(1, 3, 4), keepdims=True)
    g = g - avgs
    p = g.reshape(B, C, K, K, H, Wd)
    O = w.shape[0]
    wm = w.reshape(O, C // UM, UM, K, K).transpose(0, 4, 3, 2, 1).reshape(O, K * K * C)
    pm = p.reshape(B, C // UM, UM, K, K, H, Wd).transpose(0, 3, 4, 2, 1, 5, 6).reshape(B, K * K * C, H * Wd)
    out = (mxq(wm, 1, "e4m3") @ mxq(pm, 1, "e4m3")).reshape(B, O, H, Wd) + b[None, :, None, None]
    out = np.where(out > 0, out, SLOPE * out)
    m = avgs[:, :, :, 0, 0]
    out = out.reshape(B, O // UM, UM, H, Wd) + m
    return out.reshape(B, O, H, Wd)

@@ -1,0 +1,255 @@
+from contextlib import ExitStack
+
+import concourse.bass as bass
+import concourse.mybir as mybir
+import concourse.tile as tile
+from concourse.masks import make_identity
+
+F32 = mybir.dt.float32
+BF16 = mybir.dt.bfloat16
+U32 = mybir.dt.uint32
+U8 = mybir.dt.uint8
+FP8X4 = mybir.dt.float8_e4m3fn_x4
+ALU = mybir.AluOpType
+ACT = mybir.ActivationFunctionType
+
+FLOPS = 2 * 512 * 4608 * 2048
+
+P = 128
+BLOCKS = [
+    (0, 0, 8, "v"), (0, 12, 4, "s"), (0, 28, 4, "g"), (0, 16, 4, "s"),
+    (0, 8, 4, "v"), (0, 20, 4, "s"), (0, 24, 4, "s"),
+    (1, 0, 8, "v"), (1, 12, 4, "s"), (1, 24, 4, "g"), (1, 16, 4, "s"),
+    (1, 8, 4, "v"), (1, 28, 4, "g"), (1, 20, 4, "s"),
+]
+WPRE = "sgvv"
+STAT_ENG = "vg"
+
+
+def tile_conv2d_kernel(tc, xx, w, b, out):
+    nc = tc.nc
+    with ExitStack() as ctx:
+        const = ctx.enter_context(tc.tile_pool(name="const", bufs=1))
+        xpool = ctx.enter_context(tc.tile_pool(name="xpool", bufs=2))
+        wpool = ctx.enter_context(tc.tile_pool(name="wpool", bufs=2))
+        stat = ctx.enter_context(tc.tile_pool(name="stat", bufs=1))
+        work = ctx.enter_context(tc.tile_pool(name="work", bufs=2))
+        psum = ctx.enter_context(tc.psum_pool(name="psum", bufs=1))
+
+        xraw = []
+        for n in range(2):
+            xr = xpool.tile([P, 4, 1024], BF16, name="xraw%d" % n, tag="xraw", bufs=2)
+            xraw.append(xr)
+        xv0 = xx[0].rearrange("(t q m) h w -> m q t (h w)", t=4, q=64, m=2)
+        xv1 = xx[1].rearrange("(t q m) h w -> m q t (h w)", t=4, q=64, m=2)
+        wv = w.rearrange("o c a b -> o (c a b)")
+        nc.sync.dma_start(out=xraw[0][0:64, :, :], in_=xv0[0])
+        nc.scalar.dma_start(out=xraw[0][64:128, :, :], in_=xv0[1])
+        wsb = []
+
+        def load_w(ot):
+            ws_t = wpool.tile([P, 4608], BF16, name="wsb%d" % ot, tag="wsb", bufs=3)
+            nc.sync.dma_start(out=ws_t[:], in_=wv[128 * ot:128 * ot + 128, :])
+            wsb.append(ws_t)
+
+        for ot in range(3):
+            load_w(ot)
+        nc.sync.dma_start(out=xraw[1][0:64, :, :], in_=xv1[0])
+        nc.sync.dma_start(out=xraw[1][64:128, :, :], in_=xv1[1])
+        b_bf = const.tile([P, 4], BF16, name="b_bf")
+        bv = b.rearrange("(a q h) -> h q a", a=4, q=64, h=2)
+        with nc.allow_non_contiguous_dma(reason="512 bias values, one per partition and tile"):
+            nc.scalar.dma_start(out=b_bf[0:64, :], in_=bv[0])
+            nc.scalar.dma_start(out=b_bf[64:128, :], in_=bv[1])
+
+        ident = const.tile([P, P], F32, name="ident")
+        make_identity(nc, ident[:])
+        perm = const.tile([P, P], F32, name="perm")
+        nc.vector.tensor_copy(
+            out=perm[:].rearrange("p (h q) -> p h q", h=2),
+            in_=ident[:].rearrange("p (q h) -> p h q", h=2),
+        )
+        sel = const.tile([P, P], BF16, name="sel")
+        nc.vector.memset(sel[:], 0.0)
+        nc.vector.memset(sel[0:64, 0:64], 1.0)
+        nc.vector.memset(sel[64:128, 64:128], 1.0)
+        b32 = const.tile([P, 4], F32, name="b32")
+        nc.vector.tensor_copy(out=b32[:], in_=b_bf[:])
+        b001 = const.tile([P, 4], F32, name="b001")
+        nc.vector.tensor_scalar_mul(out=b001[:], in0=b32[:], scalar1=0.01)
+
+        WC = const.tile([P, 4, 9, P], U32, name="WC", align_bytes=64)
+        WS = const.tile([P, 4, 9, P], U8, name="WS", align_bytes=64)
+
+        XP = []
+        NV = []
+        for n in range(2):
+            xp_t = const.tile([P, 34, 34, 4], BF16, name="XP%d" % n)
+            XP.append(xp_t)
+            nv_t = const.tile([P, 32, 32], F32, name="NV%d" % n)
+            NV.append(nv_t)
+
+        def copy_on(eng, out_ap, in_ap):
+            if eng == "v":
+                nc.vector.tensor_copy(out=out_ap, in_=in_ap)
+            elif eng == "g":
+                nc.gpsimd.tensor_scalar(out=out_ap, in0=in_ap, scalar1=1.0, scalar2=0.0,
+                                        op0=ALU.mult, op1=ALU.add)
+            else:
+                nc.scalar.copy(out=out_ap, in_=in_ap)
+
+        def add_on(eng, out_ap, a_ap, b_ap):
+            if eng == "v":
+                nc.vector.tensor_tensor(out=out_ap, in0=a_ap, in1=b_ap, op=ALU.add)
+            else:
+                nc.gpsimd.tensor_tensor(out=out_ap, in0=a_ap, in1=b_ap, op=ALU.add)
+
+        def stats(n):
+            eng = STAT_ENG[n]
+            xp = XP[n]
+            copy_on(eng, xp[:, 1:33, 1:33, :], xraw[n][:].rearrange("p t (i j) -> p i j t", i=32))
+            copy_on(eng, xp[:, 1:33, 0:1, :], xp[:, 1:33, 1:2, :])
+            copy_on(eng, xp[:, 1:33, 33:34, :], xp[:, 1:33, 32:33, :])
+            copy_on(eng, xp[:, 0:1, :, :], xp[:, 1:2, :, :])
+            copy_on(eng, xp[:, 33:34, :, :], xp[:, 32:33, :, :])
+            sp = stat.tile([P, 32, 34], F32, name="sp%d" % n, tag="sp")
+            for h in range(2):
+                ssum = psum.tile([P, 16, 32], F32, name="ssum", tag="tr", bufs=3)
+                for t in range(4):
+                    nc.tensor.matmul(out=ssum[:].rearrange("p i j -> p (i j)"), lhsT=sel[:],
+                                     rhs=xraw[n][:, t, 512 * h:512 * h + 512],
+                                     start=(t == 0), stop=(t == 3))
+                rows = slice(16 * h, 16 * h + 16)
+                nc.scalar.activation(out=sp[:, rows, 1:33], in_=ssum[:], func=ACT.Copy,
+                                     scale=-1.0 / 2304.0)
+                nc.scalar.activation(out=sp[:, rows, 0:1], in_=ssum[:, :, 0:1], func=ACT.Copy,
+                                     scale=-1.0 / 2304.0)
+                nc.scalar.activation(out=sp[:, rows, 33:34], in_=ssum[:, :, 31:32], func=ACT.Copy,
+                                     scale=-1.0 / 2304.0)
+            h1 = stat.tile([P, 32, 32], F32, name="h1_%d" % n, tag="h1")
+            hp = stat.tile([P, 34, 32], F32, name="hp%d" % n, tag="hp")
+            a1 = stat.tile([P, 32, 32], F32, name="a1_%d" % n, tag="a1")
+            add_on(eng, h1[:], sp[:, :, 0:32], sp[:, :, 1:33])
+            add_on(eng, hp[:, 1:33, :], h1[:], sp[:, :, 2:34])
+            copy_on(eng, hp[:, 0:1, :], hp[:, 1:2, :])
+            copy_on(eng, hp[:, 33:34, :], hp[:, 32:33, :])
+            add_on(eng, a1[:], hp[:, 0:32, :], hp[:, 1:33, :])
+            add_on(eng, NV[n][:], a1[:], hp[:, 2:34, :])
+
+        def wprep(ot):
+            eng = WPRE[ot]
+            wview = wsb[ot][:].rearrange("o (u e q m r) -> o r u m q e", u=2, e=2, q=64, m=2, r=9)
+            for g0, R in ((0, 4), (4, 4), (8, 1)):
+                wr = wpool.tile([P, R, 2, 2, 64, 2], BF16, name="wr", tag="wr", bufs=2)
+                for k in range(R):
+                    if eng == "v":
+                        nc.vector.tensor_copy(out=wr[:, k, :, :, :, :], in_=wview[:, g0 + k, :, :, :, :])
+                    else:
+                        for u in range(2):
+                            copy_on(eng, wr[:, k, u, :, :, :], wview[:, g0 + k, u, :, :, :])
+                wg = wpool.tile([P, R * 512], BF16, name="wg", tag="wg", bufs=2, align_bytes=64)
+                wrf = wr[:].rearrange("o r u m q e -> o (r u m q e)").bitcast(F32).rearrange(
+                    "o (r u p) -> o r u p", r=R, u=2)
+                wgf = wg[:].bitcast(F32).rearrange("p (r o u) -> p r o u", r=R, u=2)
+                for k0 in range(0, R, 2):
+                    RR = min(2, R - k0)
+                    tp = psum.tile([P, 2, RR, P], F32, name="tp", tag="tr", bufs=3)
+                    for rr in range(RR):
+                        for u in range(2):
+                            nc.tensor.transpose(tp[:, u, rr, :], wrf[:, k0 + rr, u, :], perm[:])
+                    nc.scalar.copy(out=wgf[:, k0:k0 + RR, :, :], in_=tp[:].rearrange("p u r o -> p r o u"))
+                nc.vector.quantize_mx(
+                    out=WC[:, ot, g0:g0 + R, :].rearrange("p r o -> p (r o)").bitcast(FP8X4),
+                    scales=WS[:, ot, g0:g0 + R, :].rearrange("p r o -> p (r o)"),
+                    in_=wg[:],
+                )
+
+        def block(n, r0, nr, eng):
+            N = 32 * nr
+            pc = work.tile([P, 9, N], U32, name="pc", tag="pc%d" % N, bufs=(2 if N == 256 else 3),
+                           align_bytes=64)
+            ps = work.tile([P, 9, N], U8, name="ps", tag="ps%d" % N, bufs=(2 if N == 256 else 3),
+                           align_bytes=64)
+            if eng == "v":
+                nvp = psum.tile([P, nr, 32], F32, name="nvp", tag="nv", bufs=1)
+                nc.tensor.matmul(out=nvp[:].rearrange("p i j -> p (i j)"), lhsT=ident[:],
+                                 rhs=NV[n][:, r0:r0 + nr, :].rearrange("p i j -> p (i j)"),
+                                 start=True, stop=True)
+                prev = None
+                for off in range(9):
+                    u, v = divmod(off, 3)
+                    pg = work.tile([P, nr, 32, 4], BF16, name="pgv", tag="pgv%d" % N, bufs=3,
+                                   align_bytes=64)
+                    nc.vector.tensor_tensor(
+                        out=pg[:], in0=XP[n][:, r0 + u:r0 + u + nr, v:v + 32, :],
+                        in1=nvp[:].unsqueeze(3).to_broadcast([P, nr, 32, 4]), op=ALU.add)
+                    if prev is not None:
+                        nc.vector.quantize_mx(out=pc[:, off - 1, :].bitcast(FP8X4), scales=ps[:, off - 1, :],
+                                              in_=prev[:].rearrange("p i j t -> p (i j t)"))
+                    prev = pg
+                nc.vector.quantize_mx(out=pc[:, 8, :].bitcast(FP8X4), scales=ps[:, 8, :],
+                                      in_=prev[:].rearrange("p i j t -> p (i j t)"))
+            else:
+                pgall = work.tile([P, 9, N, 4], BF16, name="pg" + eng, tag="pg" + eng, bufs=2,
+                                  align_bytes=64)
+                if eng == "g":
+                    for off in range(9):
+                        u, v = divmod(off, 3)
+                        nc.gpsimd.tensor_tensor(
+                            out=pgall[:, off, :, :].rearrange("p (i j) t -> p i j t", i=nr),
+                            in0=XP[n][:, r0 + u:r0 + u + nr, v:v + 32, :],
+                            in1=NV[n][:, r0:r0 + nr, :].unsqueeze(3).to_broadcast([P, nr, 32, 4]),
+                            op=ALU.add)
+                else:
+                    for ii in range(nr):
+                        for j in range(32):
+                            i = r0 + ii
+                            nc.scalar.activation(
+                                out=pgall[:, :, ii * 32 + j, :].rearrange("p (u v) t -> p u v t", u=3),
+                                in_=XP[n][:, i:i + 3, j:j + 3, :], func=ACT.Identity,
+                                bias=NV[n][:, i, j:j + 1], scale=1.0)
+                nc.vector.quantize_mx(
+                    out=pc[:, 0:8, :].rearrange("p a x -> p (a x)").bitcast(FP8X4),
+                    scales=ps[:, 0:8, :].rearrange("p a x -> p (a x)"),
+                    in_=pgall[:, 0:8, :, :].rearrange("p a x t -> p (a x t)"))
+                nc.vector.quantize_mx(
+                    out=pc[:, 8, :].bitcast(FP8X4), scales=ps[:, 8, :],
+                    in_=pgall[:, 8, :, :].rearrange("p x t -> p (x t)"))
+
+            per_bank = 512 // N
+            accs = []
+            for ot in range(4):
+                if ot % per_bank == 0:
+                    acc = psum.tile([P, per_bank, N], F32, name="acc", tag="acc", bufs=4)
+                a = acc[:, ot % per_bank, :]
+                accs.append(a)
+                for off in range(9):
+                    u, v = divmod(off, 3)
+                    ro = 3 * v + u
+                    nc.tensor.matmul_mx(
+                        out=a, lhsT=WC[:, ot, ro, :].bitcast(FP8X4), lhsT_scale=WS[:, ot, ro, :],
+                        rhs=pc[:, off, :].bitcast(FP8X4), rhs_scale=ps[:, off, :],
+                        start=(off == 0), stop=(off == 8))
+            res = work.tile([P, 4, N], F32, name="res", tag="res%d" % N, bufs=(2 if N == 256 else 4))
+            for ot in range(4):
+                nc.scalar.activation(out=res[:, ot, :], in_=accs[ot], func=ACT.Identity,
+                                     bias=b001[:, ot:ot + 1], scale=0.01)
+            for ot in range(4):
+                nc.vector.scalar_tensor_tensor(out=res[:, ot, :], in0=accs[ot], scalar=b32[:, ot:ot + 1],
+                                               in1=res[:, ot, :], op0=ALU.add, op1=ALU.max)
+            nc.gpsimd.tensor_tensor(
+                out=res[:], in0=res[:],
+                in1=NV[n][:, r0:r0 + nr, :].rearrange("p i j -> p (i j)").unsqueeze(1).to_broadcast([P, 4, N]),
+                op=ALU.subtract)
+            ov = out[n].rearrange("(a q h) i j -> h q a (i j)", a=4, q=64, h=2)
+            for h in range(2):
+                nc.sync.dma_start(out=ov[h][:, :, 32 * r0:32 * r0 + N], in_=res[64 * h:64 * h + 64, :, :])
+
+        stats(0)
+        wprep(0)
+        load_w(3)
+        for ot in range(1, 4):
+            wprep(ot)
+        stats(1)
+        for blk in BLOCKS:
+            block(blk[0], blk[1], blk[2], blk[3])

@@ -1,8 +1,6 @@
 from contextlib import ExitStack
 
-import concourse.bass as bass
 import concourse.mybir as mybir
-import concourse.tile as tile
 from concourse.masks import make_identity
 
 F32 = mybir.dt.float32
@@ -16,14 +14,14 @@ ACT = mybir.ActivationFunctionType
 FLOPS = 2 * 512 * 4608 * 2048
 
 P = 128
+FIRST = (0, 0, 8, "v", "g")
 BLOCKS = [
-    (0, 0, 8, "v"), (0, 12, 4, "s"), (0, 28, 4, "g"), (0, 16, 4, "s"),
-    (0, 8, 4, "v"), (0, 20, 4, "s"), (0, 24, 4, "s"),
-    (1, 0, 8, "v"), (1, 12, 4, "s"), (1, 24, 4, "g"), (1, 16, 4, "s"),
-    (1, 8, 4, "v"), (1, 28, 4, "g"), (1, 20, 4, "s"),
+    (0, 20, 4, "p", "g"), (0, 28, 4, "g", "g"), (0, 8, 8, "v", "g"), (0, 24, 4, "p", "g"),
+    (0, 16, 4, "v", "g"),
+    (1, 0, 8, "v", "g"), (1, 20, 4, "p", "g"), (1, 28, 4, "g", "g"), (1, 8, 8, "v", "g"),
+    (1, 24, 4, "p", "v"), (1, 16, 4, "v", "v"),
 ]
-WPRE = "sgvv"
-STAT_ENG = "vg"
+WPRE = "sssg"
 
 
 def tile_conv2d_kernel(tc, xx, w, b, out):
@@ -43,8 +41,10 @@ def tile_conv2d_kernel(tc, xx, w, b, out):
         xv0 = xx[0].rearrange("(t q m) h w -> m q t (h w)", t=4, q=64, m=2)
         xv1 = xx[1].rearrange("(t q m) h w -> m q t (h w)", t=4, q=64, m=2)
         wv = w.rearrange("o c a b -> o (c a b)")
-        nc.sync.dma_start(out=xraw[0][0:64, :, :], in_=xv0[0])
-        nc.scalar.dma_start(out=xraw[0][64:128, :, :], in_=xv0[1])
+        for h in range(2):
+            cols = slice(512 * h, 512 * h + 512)
+            nc.sync.dma_start(out=xraw[0][0:64, :, cols], in_=xv0[0][:, :, cols])
+            nc.scalar.dma_start(out=xraw[0][64:128, :, cols], in_=xv0[1][:, :, cols])
         wsb = []
 
         def load_w(ot):
@@ -62,17 +62,19 @@ def tile_conv2d_kernel(tc, xx, w, b, out):
             nc.scalar.dma_start(out=b_bf[0:64, :], in_=bv[0])
             nc.scalar.dma_start(out=b_bf[64:128, :], in_=bv[1])
 
+        sel = const.tile([P, P], BF16, name="sel")
+        nc.vector.memset(sel[:], 0.0)
+        nc.vector.memset(sel[0:64, 0:64], 1.0)
+        nc.vector.memset(sel[64:128, 64:128], 1.0)
         ident = const.tile([P, P], F32, name="ident")
         make_identity(nc, ident[:])
+        identb = const.tile([P, P], BF16, name="identb")
+        nc.vector.tensor_copy(out=identb[:], in_=ident[:])
         perm = const.tile([P, P], F32, name="perm")
         nc.vector.tensor_copy(
             out=perm[:].rearrange("p (h q) -> p h q", h=2),
             in_=ident[:].rearrange("p (q h) -> p h q", h=2),
         )
-        sel = const.tile([P, P], BF16, name="sel")
-        nc.vector.memset(sel[:], 0.0)
-        nc.vector.memset(sel[0:64, 0:64], 1.0)
-        nc.vector.memset(sel[64:128, 64:128], 1.0)
         b32 = const.tile([P, 4], F32, name="b32")
         nc.vector.tensor_copy(out=b32[:], in_=b_bf[:])
         b001 = const.tile([P, 4], F32, name="b001")
@@ -84,7 +86,7 @@ def tile_conv2d_kernel(tc, xx, w, b, out):
         XP = []
         NV = []
         for n in range(2):
-            xp_t = const.tile([P, 34, 34, 4], BF16, name="XP%d" % n)
+            xp_t = const.tile([P, 34, 36, 4], BF16, name="XP%d" % n)
             XP.append(xp_t)
             nv_t = const.tile([P, 32, 32], F32, name="NV%d" % n)
             NV.append(nv_t)
@@ -104,37 +106,54 @@ def tile_conv2d_kernel(tc, xx, w, b, out):
             else:
                 nc.gpsimd.tensor_tensor(out=out_ap, in0=a_ap, in1=b_ap, op=ALU.add)
 
-        def stats(n):
-            eng = STAT_ENG[n]
+        def pad_half(n, h, eng):
             xp = XP[n]
-            copy_on(eng, xp[:, 1:33, 1:33, :], xraw[n][:].rearrange("p t (i j) -> p i j t", i=32))
-            copy_on(eng, xp[:, 1:33, 0:1, :], xp[:, 1:33, 1:2, :])
-            copy_on(eng, xp[:, 1:33, 33:34, :], xp[:, 1:33, 32:33, :])
-            copy_on(eng, xp[:, 0:1, :, :], xp[:, 1:2, :, :])
-            copy_on(eng, xp[:, 33:34, :, :], xp[:, 32:33, :, :])
-            sp = stat.tile([P, 32, 34], F32, name="sp%d" % n, tag="sp")
-            for h in range(2):
-                ssum = psum.tile([P, 16, 32], F32, name="ssum", tag="tr", bufs=3)
-                for t in range(4):
-                    nc.tensor.matmul(out=ssum[:].rearrange("p i j -> p (i j)"), lhsT=sel[:],
-                                     rhs=xraw[n][:, t, 512 * h:512 * h + 512],
-                                     start=(t == 0), stop=(t == 3))
-                rows = slice(16 * h, 16 * h + 16)
-                nc.scalar.activation(out=sp[:, rows, 1:33], in_=ssum[:], func=ACT.Copy,
-                                     scale=-1.0 / 2304.0)
-                nc.scalar.activation(out=sp[:, rows, 0:1], in_=ssum[:, :, 0:1], func=ACT.Copy,
-                                     scale=-1.0 / 2304.0)
-                nc.scalar.activation(out=sp[:, rows, 33:34], in_=ssum[:, :, 31:32], func=ACT.Copy,
-                                     scale=-1.0 / 2304.0)
-            h1 = stat.tile([P, 32, 32], F32, name="h1_%d" % n, tag="h1")
-            hp = stat.tile([P, 34, 32], F32, name="hp%d" % n, tag="hp")
-            a1 = stat.tile([P, 32, 32], F32, name="a1_%d" % n, tag="a1")
-            add_on(eng, h1[:], sp[:, :, 0:32], sp[:, :, 1:33])
-            add_on(eng, hp[:, 1:33, :], h1[:], sp[:, :, 2:34])
-            copy_on(eng, hp[:, 0:1, :], hp[:, 1:2, :])
-            copy_on(eng, hp[:, 33:34, :], hp[:, 32:33, :])
-            add_on(eng, a1[:], hp[:, 0:32, :], hp[:, 1:33, :])
-            add_on(eng, NV[n][:], a1[:], hp[:, 2:34, :])
+            rows = slice(1 + 16 * h, 17 + 16 * h)
+            copy_on(eng, xp[:, rows, 1:33, :],
+                    xraw[n][:, :, 512 * h:512 * h + 512].rearrange("p t (i j) -> p i j t", i=16))
+            copy_on(eng, xp[:, rows, 0:1, :], xp[:, rows, 1:2, :])
+            copy_on(eng, xp[:, rows, 33:34, :], xp[:, rows, 32:33, :])
+            if h == 0:
+                copy_on(eng, xp[:, 0:1, 0:34, :], xp[:, 1:2, 0:34, :])
+            else:
+                copy_on(eng, xp[:, 33:34, 0:34, :], xp[:, 32:33, 0:34, :])
+
+        st = {}
+
+        def stat_tiles(n):
+            st["sp"] = stat.tile([P, 32, 34], F32, name="sp%d" % n, tag="sp")
+            st["h1"] = stat.tile([P, 32, 32], F32, name="h1x%d" % n, tag="h1")
+            st["hp"] = stat.tile([P, 34, 32], F32, name="hp%d" % n, tag="hp")
+            st["a1"] = stat.tile([P, 32, 32], F32, name="a1x%d" % n, tag="a1")
+
+        def sum_half(n, h):
+            sp = st["sp"]
+            ssum = psum.tile([P, 16, 32], F32, name="ssum", tag="tr", bufs=3)
+            for t in range(4):
+                nc.tensor.matmul(out=ssum[:].rearrange("p i j -> p (i j)"), lhsT=sel[:],
+                                 rhs=xraw[n][:, t, 512 * h:512 * h + 512],
+                                 start=(t == 0), stop=(t == 3))
+            rows = slice(16 * h, 16 * h + 16)
+            nc.scalar.activation(out=sp[:, rows, 1:33], in_=ssum[:], func=ACT.Copy, scale=-1.0 / 2304.0)
+            nc.scalar.activation(out=sp[:, rows, 0:1], in_=ssum[:, :, 0:1], func=ACT.Copy,
+                                 scale=-1.0 / 2304.0)
+            nc.scalar.activation(out=sp[:, rows, 33:34], in_=ssum[:, :, 31:32], func=ACT.Copy,
+                                 scale=-1.0 / 2304.0)
+
+        def box_h(n, h, eng):
+            sp, h1, hp = st["sp"], st["h1"], st["hp"]
+            rows = slice(16 * h, 16 * h + 16)
+            add_on(eng, h1[:, rows, :], sp[:, rows, 0:32], sp[:, rows, 1:33])
+            add_on(eng, hp[:, 1 + 16 * h:17 + 16 * h, :], h1[:, rows, :], sp[:, rows, 2:34])
+            if h == 0:
+                copy_on(eng, hp[:, 0:1, :], hp[:, 1:2, :])
+            else:
+                copy_on(eng, hp[:, 33:34, :], hp[:, 32:33, :])
+
+        def box_v(n, lo, hi, eng):
+            hp, a1 = st["hp"], st["a1"]
+            add_on(eng, a1[:, lo:hi, :], hp[:, lo:hi, :], hp[:, lo + 1:hi + 1, :])
+            add_on(eng, NV[n][:, lo:hi, :], a1[:, lo:hi, :], hp[:, lo + 2:hi + 2, :])
 
         def wprep(ot):
             eng = WPRE[ot]
@@ -164,34 +183,38 @@ def tile_conv2d_kernel(tc, xx, w, b, out):
                     in_=wg[:],
                 )
 
-        def block(n, r0, nr, eng):
+        def quant(pc, ps, lo, hi, src):
+            nc.vector.quantize_mx(
+                out=pc[:, lo:hi, :].rearrange("p a x -> p (a x)").bitcast(FP8X4),
+                scales=ps[:, lo:hi, :].rearrange("p a x -> p (a x)"),
+                in_=src.rearrange("p a x t -> p (a x t)"))
+
+        def block_a(n, r0, nr, eng):
             N = 32 * nr
-            pc = work.tile([P, 9, N], U32, name="pc", tag="pc%d" % N, bufs=(2 if N == 256 else 3),
-                           align_bytes=64)
-            ps = work.tile([P, 9, N], U8, name="ps", tag="ps%d" % N, bufs=(2 if N == 256 else 3),
-                           align_bytes=64)
+            nb = 2 if N == 256 else 3
+            pc = work.tile([P, 9, N], U32, name="pc", tag="pc%d" % N, bufs=nb, align_bytes=64)
+            ps = work.tile([P, 9, N], U8, name="ps", tag="ps%d" % N, bufs=nb, align_bytes=64)
             if eng == "v":
                 nvp = psum.tile([P, nr, 32], F32, name="nvp", tag="nv", bufs=1)
                 nc.tensor.matmul(out=nvp[:].rearrange("p i j -> p (i j)"), lhsT=ident[:],
                                  rhs=NV[n][:, r0:r0 + nr, :].rearrange("p i j -> p (i j)"),
                                  start=True, stop=True)
-                prev = None
+                pga = work.tile([P, 4, N, 4], BF16, name="pga", tag="pga", bufs=1, align_bytes=64)
+                pgb = work.tile([P, 4, N, 4], BF16, name="pgb", tag="pgb", bufs=1, align_bytes=64)
+                pgc = work.tile([P, 1, N, 4], BF16, name="pgc", tag="pgc", bufs=1, align_bytes=64)
+                dst = [pga, pgb, pgc]
                 for off in range(9):
                     u, v = divmod(off, 3)
-                    pg = work.tile([P, nr, 32, 4], BF16, name="pgv", tag="pgv%d" % N, bufs=3,
-                                   align_bytes=64)
                     nc.vector.tensor_tensor(
-                        out=pg[:], in0=XP[n][:, r0 + u:r0 + u + nr, v:v + 32, :],
+                        out=dst[off // 4][:, off % 4, :, :].rearrange("p (i j) t -> p i j t", i=nr),
+                        in0=XP[n][:, r0 + u:r0 + u + nr, v:v + 32, :],
                         in1=nvp[:].unsqueeze(3).to_broadcast([P, nr, 32, 4]), op=ALU.add)
-                    if prev is not None:
-                        nc.vector.quantize_mx(out=pc[:, off - 1, :].bitcast(FP8X4), scales=ps[:, off - 1, :],
-                                              in_=prev[:].rearrange("p i j t -> p (i j t)"))
-                    prev = pg
-                nc.vector.quantize_mx(out=pc[:, 8, :].bitcast(FP8X4), scales=ps[:, 8, :],
-                                      in_=prev[:].rearrange("p i j t -> p (i j t)"))
+                quant(pc, ps, 0, 4, pga[:])
+                quant(pc, ps, 4, 8, pgb[:])
+                quant(pc, ps, 8, 9, pgc[:])
             else:
-                pgall = work.tile([P, 9, N, 4], BF16, name="pg" + eng, tag="pg" + eng, bufs=2,
-                                  align_bytes=64)
+                pgall = work.tile([P, 9, N, 4], BF16, name="pg" + eng, tag="pg" + eng,
+                                  bufs=(1 if eng == "g" else 2), align_bytes=64)
                 if eng == "g":
                     for off in range(9):
                         u, v = divmod(off, 3)
@@ -201,21 +224,27 @@ def tile_conv2d_kernel(tc, xx, w, b, out):
                             in1=NV[n][:, r0:r0 + nr, :].unsqueeze(3).to_broadcast([P, nr, 32, 4]),
                             op=ALU.add)
                 else:
-                    for ii in range(nr):
-                        for j in range(32):
-                            i = r0 + ii
-                            nc.scalar.activation(
-                                out=pgall[:, :, ii * 32 + j, :].rearrange("p (u v) t -> p u v t", u=3),
-                                in_=XP[n][:, i:i + 3, j:j + 3, :], func=ACT.Identity,
-                                bias=NV[n][:, i, j:j + 1], scale=1.0)
-                nc.vector.quantize_mx(
-                    out=pc[:, 0:8, :].rearrange("p a x -> p (a x)").bitcast(FP8X4),
-                    scales=ps[:, 0:8, :].rearrange("p a x -> p (a x)"),
-                    in_=pgall[:, 0:8, :, :].rearrange("p a x t -> p (a x t)"))
-                nc.vector.quantize_mx(
-                    out=pc[:, 8, :].bitcast(FP8X4), scales=ps[:, 8, :],
-                    in_=pgall[:, 8, :, :].rearrange("p x t -> p (x t)"))
+                    ta = psum.tile([P, P], F32, name="ta", tag="tr", bufs=3)
+                    nc.tensor.transpose(ta[:], NV[n][:, r0:r0 + nr, :].rearrange("p i j -> p (i j)"),
+                                        ident[:])
+                    a2 = work.tile([P, P], F32, name="a2", tag="a2", bufs=2)
+                    nc.scalar.copy(out=a2[:], in_=ta[:])
+                    for off in range(9):
+                        u, v = divmod(off, 3)
+                        pp = psum.tile([P, 4, N], F32, name="pp", tag="tr", bufs=3)
+                        for t in range(4):
+                            nc.tensor.matmul(out=pp[:, t, :], lhsT=a2[:], rhs=ident[:], is_transpose=True,
+                                             start=(t == 0), stop=False)
+                        nc.tensor.matmul(out=pp[:].rearrange("p t (i j) -> p i j t", i=nr), lhsT=identb[:],
+                                         rhs=XP[n][:, r0 + u:r0 + u + nr, v:v + 32, :],
+                                         start=False, stop=True)
+                        nc.scalar.copy(out=pgall[:, off, :, :], in_=pp[:].rearrange("p t x -> p x t"))
+                quant(pc, ps, 0, 8, pgall[:, 0:8, :, :])
+                quant(pc, ps, 8, 9, pgall[:, 8:9, :, :])
+            return pc, ps
 
+        def block_b(n, r0, nr, last, pc, ps):
+            N = 32 * nr
             per_bank = 512 // N
             accs = []
             for ot in range(4):
@@ -230,26 +259,44 @@ def tile_conv2d_kernel(tc, xx, w, b, out):
                         out=a, lhsT=WC[:, ot, ro, :].bitcast(FP8X4), lhsT_scale=WS[:, ot, ro, :],
                         rhs=pc[:, off, :].bitcast(FP8X4), rhs_scale=ps[:, off, :],
                         start=(off == 0), stop=(off == 8))
-            res = work.tile([P, 4, N], F32, name="res", tag="res%d" % N, bufs=(2 if N == 256 else 4))
+            res = work.tile([P, 4, N], F32, name="res", tag="res%d" % N, bufs=(2 if N == 256 else 3))
             for ot in range(4):
                 nc.scalar.activation(out=res[:, ot, :], in_=accs[ot], func=ACT.Identity,
                                      bias=b001[:, ot:ot + 1], scale=0.01)
             for ot in range(4):
                 nc.vector.scalar_tensor_tensor(out=res[:, ot, :], in0=accs[ot], scalar=b32[:, ot:ot + 1],
                                                in1=res[:, ot, :], op0=ALU.add, op1=ALU.max)
-            nc.gpsimd.tensor_tensor(
-                out=res[:], in0=res[:],
-                in1=NV[n][:, r0:r0 + nr, :].rearrange("p i j -> p (i j)").unsqueeze(1).to_broadcast([P, 4, N]),
-                op=ALU.subtract)
+            nvb = NV[n][:, r0:r0 + nr, :].rearrange("p i j -> p (i j)").unsqueeze(1).to_broadcast([P, 4, N])
+            if last == "g":
+                nc.gpsimd.tensor_tensor(out=res[:], in0=res[:], in1=nvb, op=ALU.subtract)
+            else:
+                nc.vector.tensor_tensor(out=res[:], in0=res[:], in1=nvb, op=ALU.subtract)
             ov = out[n].rearrange("(a q h) i j -> h q a (i j)", a=4, q=64, h=2)
             for h in range(2):
                 nc.sync.dma_start(out=ov[h][:, :, 32 * r0:32 * r0 + N], in_=res[64 * h:64 * h + 64, :, :])
 
-        stats(0)
+        stat_tiles(0)
+        pad_half(0, 0, "v")
+        sum_half(0, 0)
+        box_h(0, 0, "v")
+        box_v(0, 0, 15, "v")
+        sum_half(0, 1)
+        pad_half(0, 1, "s")
+        box_h(0, 1, "v")
+        box_v(0, 15, 32, "v")
+        pc0, ps0 = block_a(FIRST[0], FIRST[1], FIRST[2], FIRST[3])
         wprep(0)
         load_w(3)
         for ot in range(1, 4):
             wprep(ot)
-        stats(1)
+        stat_tiles(1)
+        for h in range(2):
+            sum_half(1, h)
+            box_h(1, h, "g")
+        box_v(1, 0, 32, "g")
+        for h in range(2):
+            pad_half(1, h, "s")
+        block_b(FIRST[0], FIRST[1], FIRST[2], FIRST[4], pc0, ps0)
         for blk in BLOCKS:
-            block(blk[0], blk[1], blk[2], blk[3])
+            pcx, psx = block_a(blk[0], blk[1], blk[2], blk[3])
+            block_b(blk[0], blk[1], blk[2], blk[4], pcx, psx)

@@ -16,12 +16,11 @@ FLOPS = 2 * 512 * 4608 * 2048
 P = 128
 FIRST = (0, 0, 8, "v", "g")
 BLOCKS = [
-    (0, 20, 4, "p", "g"), (0, 28, 4, "g", "g"), (0, 8, 8, "v", "g"), (0, 24, 4, "p", "g"),
-    (0, 16, 4, "v", "g"),
-    (1, 0, 8, "v", "g"), (1, 20, 4, "p", "g"), (1, 28, 4, "g", "g"), (1, 8, 8, "v", "g"),
-    (1, 24, 4, "p", "v"), (1, 16, 4, "v", "v"),
+    (0, 24, 4, "p", "g"), (0, 8, 8, "v", "g"), (0, 28, 4, "p", "g"), (0, 16, 8, "v", "g"),
+    (1, 0, 8, "v", "g"), (1, 24, 4, "p", "g"), (1, 8, 8, "v", "g"), (1, 28, 4, "p", "g"),
+    (1, 16, 4, "v", "v"), (1, 20, 4, "v", "v"),
 ]
-WPRE = "sssg"
+WPRE = "svsv"
 
 
 def tile_conv2d_kernel(tc, xx, w, b, out):
@@ -79,6 +78,8 @@ def tile_conv2d_kernel(tc, xx, w, b, out):
         nc.vector.tensor_copy(out=b32[:], in_=b_bf[:])
         b001 = const.tile([P, 4], F32, name="b001")
         nc.vector.tensor_scalar_mul(out=b001[:], in0=b32[:], scalar1=0.01)
+        b099 = const.tile([P, 4], F32, name="b099")
+        nc.vector.tensor_scalar_mul(out=b099[:], in0=b32[:], scalar1=0.99)
 
         WC = const.tile([P, 4, 9, P], U32, name="WC", align_bytes=64)
         WS = const.tile([P, 4, 9, P], U8, name="WS", align_bytes=64)
@@ -260,17 +261,19 @@ def tile_conv2d_kernel(tc, xx, w, b, out):
                         rhs=pc[:, off, :].bitcast(FP8X4), rhs_scale=ps[:, off, :],
                         start=(off == 0), stop=(off == 8))
             res = work.tile([P, 4, N], F32, name="res", tag="res%d" % N, bufs=(2 if N == 256 else 3))
+            rel = work.tile([P, 4, N], F32, name="rel", tag="rel%d" % N, bufs=(2 if N == 256 else 3))
             for ot in range(4):
                 nc.scalar.activation(out=res[:, ot, :], in_=accs[ot], func=ACT.Identity,
                                      bias=b001[:, ot:ot + 1], scale=0.01)
-            for ot in range(4):
-                nc.vector.scalar_tensor_tensor(out=res[:, ot, :], in0=accs[ot], scalar=b32[:, ot:ot + 1],
-                                               in1=res[:, ot, :], op0=ALU.add, op1=ALU.max)
+                nc.scalar.activation(out=rel[:, ot, :], in_=accs[ot], func=ACT.Relu,
+                                     bias=b099[:, ot:ot + 1], scale=0.99)
             nvb = NV[n][:, r0:r0 + nr, :].rearrange("p i j -> p (i j)").unsqueeze(1).to_broadcast([P, 4, N])
             if last == "g":
                 nc.gpsimd.tensor_tensor(out=res[:], in0=res[:], in1=nvb, op=ALU.subtract)
+                nc.gpsimd.tensor_tensor(out=res[:], in0=res[:], in1=rel[:], op=ALU.add)
             else:
                 nc.vector.tensor_tensor(out=res[:], in0=res[:], in1=nvb, op=ALU.subtract)
+                nc.vector.tensor_tensor(out=res[:], in0=res[:], in1=rel[:], op=ALU.add)
             ov = out[n].rearrange("(a q h) i j -> h q a (i j)", a=4, q=64, h=2)
             for h in range(2):
                 nc.sync.dma_start(out=ov[h][:, :, 32 * r0:32 * r0 + N], in_=res[64 * h:64 * h + 64, :, :])
@@ -287,13 +290,14 @@ def tile_conv2d_kernel(tc, xx, w, b, out):
         pc0, ps0 = block_a(FIRST[0], FIRST[1], FIRST[2], FIRST[3])
         wprep(0)
         load_w(3)
-        for ot in range(1, 4):
-            wprep(ot)
+        wprep(1)
         stat_tiles(1)
         for h in range(2):
             sum_half(1, h)
             box_h(1, h, "g")
         box_v(1, 0, 32, "g")
+        wprep(2)
+        wprep(3)
         for h in range(2):
             pad_half(1, h, "s")
         block_b(FIRST[0], FIRST[1], FIRST[2], FIRST[4], pc0, ps0)

@@ -14,13 +14,11 @@ ACT = mybir.ActivationFunctionType
 FLOPS = 2 * 512 * 4608 * 2048
 
 P = 128
-FIRST = (0, 0, 8, "v", "g")
 BLOCKS = [
-    (0, 24, 4, "p", "g"), (0, 8, 8, "v", "g"), (0, 28, 4, "p", "g"), (0, 16, 8, "v", "g"),
-    (1, 0, 8, "v", "g"), (1, 24, 4, "p", "g"), (1, 8, 8, "v", "g"), (1, 28, 4, "p", "g"),
-    (1, 16, 4, "v", "v"), (1, 20, 4, "v", "v"),
+    (0, 0, 16, 4, "g"), (0, 16, 16, 4, "g"), (1, 0, 16, 4, "g"), (1, 16, 8, 4, "g"), (1, 24, 8, 0, "v"),
 ]
-WPRE = "svsv"
+WPRE = "sgsg"
+SPLIT = 17
 
 
 def tile_conv2d_kernel(tc, xx, w, b, out):
@@ -40,19 +38,14 @@ def tile_conv2d_kernel(tc, xx, w, b, out):
         xv0 = xx[0].rearrange("(t q m) h w -> m q t (h w)", t=4, q=64, m=2)
         xv1 = xx[1].rearrange("(t q m) h w -> m q t (h w)", t=4, q=64, m=2)
         wv = w.rearrange("o c a b -> o (c a b)")
-        for h in range(2):
-            cols = slice(512 * h, 512 * h + 512)
+        for cols in (slice(0, 32 * SPLIT), slice(32 * SPLIT, 1024)):
             nc.sync.dma_start(out=xraw[0][0:64, :, cols], in_=xv0[0][:, :, cols])
             nc.scalar.dma_start(out=xraw[0][64:128, :, cols], in_=xv0[1][:, :, cols])
         wsb = []
-
-        def load_w(ot):
-            ws_t = wpool.tile([P, 4608], BF16, name="wsb%d" % ot, tag="wsb", bufs=3)
+        for ot in range(4):
+            ws_t = wpool.tile([P, 4608], BF16, name="wsb%d" % ot, tag="wsb", bufs=4)
             nc.sync.dma_start(out=ws_t[:], in_=wv[128 * ot:128 * ot + 128, :])
             wsb.append(ws_t)
-
-        for ot in range(3):
-            load_w(ot)
         nc.sync.dma_start(out=xraw[1][0:64, :, :], in_=xv1[0])
         nc.sync.dma_start(out=xraw[1][64:128, :, :], in_=xv1[1])
         b_bf = const.tile([P, 4], BF16, name="b_bf")
@@ -65,6 +58,8 @@ def tile_conv2d_kernel(tc, xx, w, b, out):
         nc.vector.memset(sel[:], 0.0)
         nc.vector.memset(sel[0:64, 0:64], 1.0)
         nc.vector.memset(sel[64:128, 64:128], 1.0)
+        warm = const.tile([P, 8], F32, name="warm")
+        nc.scalar.activation(out=warm[:], in_=sel[:, 0:8], func=ACT.Relu)
         ident = const.tile([P, P], F32, name="ident")
         make_identity(nc, ident[:])
         identb = const.tile([P, P], BF16, name="identb")
@@ -101,60 +96,60 @@ def tile_conv2d_kernel(tc, xx, w, b, out):
             else:
                 nc.scalar.copy(out=out_ap, in_=in_ap)
 
-        def add_on(eng, out_ap, a_ap, b_ap):
+        def tt_on(eng, out_ap, a_ap, b_ap, op):
             if eng == "v":
-                nc.vector.tensor_tensor(out=out_ap, in0=a_ap, in1=b_ap, op=ALU.add)
+                nc.vector.tensor_tensor(out=out_ap, in0=a_ap, in1=b_ap, op=op)
             else:
-                nc.gpsimd.tensor_tensor(out=out_ap, in0=a_ap, in1=b_ap, op=ALU.add)
+                nc.gpsimd.tensor_tensor(out=out_ap, in0=a_ap, in1=b_ap, op=op)
 
-        def pad_half(n, h, eng):
+        def pad_rows(n, ra, rb, eng):
             xp = XP[n]
-            rows = slice(1 + 16 * h, 17 + 16 * h)
+            rows = slice(1 + ra, 1 + rb)
             copy_on(eng, xp[:, rows, 1:33, :],
-                    xraw[n][:, :, 512 * h:512 * h + 512].rearrange("p t (i j) -> p i j t", i=16))
+                    xraw[n][:, :, 32 * ra:32 * rb].rearrange("p t (i j) -> p i j t", i=rb - ra))
             copy_on(eng, xp[:, rows, 0:1, :], xp[:, rows, 1:2, :])
             copy_on(eng, xp[:, rows, 33:34, :], xp[:, rows, 32:33, :])
-            if h == 0:
+            if ra == 0:
                 copy_on(eng, xp[:, 0:1, 0:34, :], xp[:, 1:2, 0:34, :])
-            else:
+            if rb == 32:
                 copy_on(eng, xp[:, 33:34, 0:34, :], xp[:, 32:33, 0:34, :])
 
         st = {}
 
         def stat_tiles(n):
             st["sp"] = stat.tile([P, 32, 34], F32, name="sp%d" % n, tag="sp")
-            st["h1"] = stat.tile([P, 32, 32], F32, name="h1x%d" % n, tag="h1")
+            st["tm"] = stat.tile([P, 32, 32], F32, name="tm%d" % n, tag="tm")
             st["hp"] = stat.tile([P, 34, 32], F32, name="hp%d" % n, tag="hp")
-            st["a1"] = stat.tile([P, 32, 32], F32, name="a1x%d" % n, tag="a1")
 
-        def sum_half(n, h):
+        def sums(n, ra, rb):
             sp = st["sp"]
-            ssum = psum.tile([P, 16, 32], F32, name="ssum", tag="tr", bufs=3)
-            for t in range(4):
-                nc.tensor.matmul(out=ssum[:].rearrange("p i j -> p (i j)"), lhsT=sel[:],
-                                 rhs=xraw[n][:, t, 512 * h:512 * h + 512],
-                                 start=(t == 0), stop=(t == 3))
-            rows = slice(16 * h, 16 * h + 16)
-            nc.scalar.activation(out=sp[:, rows, 1:33], in_=ssum[:], func=ACT.Copy, scale=-1.0 / 2304.0)
-            nc.scalar.activation(out=sp[:, rows, 0:1], in_=ssum[:, :, 0:1], func=ACT.Copy,
-                                 scale=-1.0 / 2304.0)
-            nc.scalar.activation(out=sp[:, rows, 33:34], in_=ssum[:, :, 31:32], func=ACT.Copy,
-                                 scale=-1.0 / 2304.0)
+            for r in range(ra, rb, 16):
+                re = min(r + 16, rb)
+                ssum = psum.tile([P, re - r, 32], F32, name="ssum", tag="tr", bufs=3)
+                for t in range(4):
+                    nc.tensor.matmul(out=ssum[:].rearrange("p i j -> p (i j)"), lhsT=sel[:],
+                                     rhs=xraw[n][:, t, 32 * r:32 * re],
+                                     start=(t == 0), stop=(t == 3))
+                nc.scalar.activation(out=sp[:, r:re, 1:33], in_=ssum[:], func=ACT.Copy,
+                                     scale=-1.0 / 2304.0)
+                nc.scalar.activation(out=sp[:, r:re, 0:1], in_=ssum[:, :, 0:1], func=ACT.Copy,
+                                     scale=-1.0 / 2304.0)
+                nc.scalar.activation(out=sp[:, r:re, 33:34], in_=ssum[:, :, 31:32], func=ACT.Copy,
+                                     scale=-1.0 / 2304.0)
 
-        def box_h(n, h, eng):
-            sp, h1, hp = st["sp"], st["h1"], st["hp"]
-            rows = slice(16 * h, 16 * h + 16)
-            add_on(eng, h1[:, rows, :], sp[:, rows, 0:32], sp[:, rows, 1:33])
-            add_on(eng, hp[:, 1 + 16 * h:17 + 16 * h, :], h1[:, rows, :], sp[:, rows, 2:34])
-            if h == 0:
+        def box_h(ra, rb, eng):
+            sp, tm, hp = st["sp"], st["tm"], st["hp"]
+            tt_on(eng, tm[:, ra:rb, :], sp[:, ra:rb, 0:32], sp[:, ra:rb, 1:33], ALU.add)
+            tt_on(eng, hp[:, 1 + ra:1 + rb, :], tm[:, ra:rb, :], sp[:, ra:rb, 2:34], ALU.add)
+            if ra == 0:
                 copy_on(eng, hp[:, 0:1, :], hp[:, 1:2, :])
-            else:
+            if rb == 32:
                 copy_on(eng, hp[:, 33:34, :], hp[:, 32:33, :])
 
         def box_v(n, lo, hi, eng):
-            hp, a1 = st["hp"], st["a1"]
-            add_on(eng, a1[:, lo:hi, :], hp[:, lo:hi, :], hp[:, lo + 1:hi + 1, :])
-            add_on(eng, NV[n][:, lo:hi, :], a1[:, lo:hi, :], hp[:, lo + 2:hi + 2, :])
+            hp, tm = st["hp"], st["tm"]
+            tt_on(eng, tm[:, lo:hi, :], hp[:, lo:hi, :], hp[:, lo + 1:hi + 1, :], ALU.add)
+            tt_on(eng, NV[n][:, lo:hi, :], tm[:, lo:hi, :], hp[:, lo + 2:hi + 2, :], ALU.add)
 
         def wprep(ot):
             eng = WPRE[ot]
@@ -184,123 +179,98 @@ def tile_conv2d_kernel(tc, xx, w, b, out):
                     in_=wg[:],
                 )
 
-        def quant(pc, ps, lo, hi, src):
-            nc.vector.quantize_mx(
-                out=pc[:, lo:hi, :].rearrange("p a x -> p (a x)").bitcast(FP8X4),
-                scales=ps[:, lo:hi, :].rearrange("p a x -> p (a x)"),
-                in_=src.rearrange("p a x t -> p (a x t)"))
-
-        def block_a(n, r0, nr, eng):
+        def block(n, r0, nr, rp, add_eng):
             N = 32 * nr
-            nb = 2 if N == 256 else 3
-            pc = work.tile([P, 9, N], U32, name="pc", tag="pc%d" % N, bufs=nb, align_bytes=64)
-            ps = work.tile([P, 9, N], U8, name="ps", tag="ps%d" % N, bufs=nb, align_bytes=64)
-            if eng == "v":
-                nvp = psum.tile([P, nr, 32], F32, name="nvp", tag="nv", bufs=1)
-                nc.tensor.matmul(out=nvp[:].rearrange("p i j -> p (i j)"), lhsT=ident[:],
-                                 rhs=NV[n][:, r0:r0 + nr, :].rearrange("p i j -> p (i j)"),
-                                 start=True, stop=True)
-                pga = work.tile([P, 4, N, 4], BF16, name="pga", tag="pga", bufs=1, align_bytes=64)
-                pgb = work.tile([P, 4, N, 4], BF16, name="pgb", tag="pgb", bufs=1, align_bytes=64)
-                pgc = work.tile([P, 1, N, 4], BF16, name="pgc", tag="pgc", bufs=1, align_bytes=64)
-                dst = [pga, pgb, pgc]
-                for off in range(9):
+            rv = nr - rp
+            pc = work.tile([P, 9, N], U32, name="pc", tag="pc", bufs=2, align_bytes=64)
+            ps = work.tile([P, 9, N], U8, name="ps", tag="ps", bufs=2, align_bytes=64)
+            nvp = psum.tile([P, rv, 32], F32, name="nvp", tag="nv", bufs=1)
+            nc.tensor.matmul(out=nvp[:].rearrange("p i j -> p (i j)"), lhsT=ident[:],
+                             rhs=NV[n][:, r0:r0 + rv, :].rearrange("p i j -> p (i j)"),
+                             start=True, stop=True)
+            a2 = None
+            if rp:
+                ta = psum.tile([P, P], F32, name="ta", tag="tr", bufs=3)
+                nc.tensor.transpose(ta[:], NV[n][:, r0 + rv:r0 + nr, :].rearrange("p i j -> p (i j)"),
+                                    ident[:])
+                a2 = work.tile([P, P], F32, name="a2", tag="a2", bufs=2)
+                nc.scalar.copy(out=a2[:], in_=ta[:])
+            accs = []
+            for ot in range(4):
+                acc = psum.tile([P, N], F32, name="acc%d" % ot, tag="acc", bufs=4)
+                accs.append(acc)
+
+            def finish(pg, grp):
+                lo, hi = grp[0], grp[-1] + 1
+                nc.vector.quantize_mx(
+                    out=pc[:, lo:hi, :].rearrange("p a x -> p (a x)").bitcast(FP8X4),
+                    scales=ps[:, lo:hi, :].rearrange("p a x -> p (a x)"),
+                    in_=pg[:, 0:hi - lo, :, :].rearrange("p a x t -> p (a x t)"))
+                for off in grp:
+                    u, v = divmod(off, 3)
+                    ro = 3 * v + u
+                    for ot in range(4):
+                        nc.tensor.matmul_mx(
+                            out=accs[ot][:], lhsT=WC[:, ot, ro, :].bitcast(FP8X4),
+                            lhsT_scale=WS[:, ot, ro, :],
+                            rhs=pc[:, off, :].bitcast(FP8X4), rhs_scale=ps[:, off, :],
+                            start=(off == 0), stop=(off == 8))
+
+            gsz = 1024 // N
+            prev = None
+            for g0 in range(0, 9, gsz):
+                grp = list(range(g0, min(g0 + gsz, 9)))
+                pg = work.tile([P, gsz, N, 4], BF16, name="pg", tag="pg", bufs=3, align_bytes=64)
+                for k, off in enumerate(grp):
                     u, v = divmod(off, 3)
                     nc.vector.tensor_tensor(
-                        out=dst[off // 4][:, off % 4, :, :].rearrange("p (i j) t -> p i j t", i=nr),
-                        in0=XP[n][:, r0 + u:r0 + u + nr, v:v + 32, :],
-                        in1=nvp[:].unsqueeze(3).to_broadcast([P, nr, 32, 4]), op=ALU.add)
-                quant(pc, ps, 0, 4, pga[:])
-                quant(pc, ps, 4, 8, pgb[:])
-                quant(pc, ps, 8, 9, pgc[:])
-            else:
-                pgall = work.tile([P, 9, N, 4], BF16, name="pg" + eng, tag="pg" + eng,
-                                  bufs=(1 if eng == "g" else 2), align_bytes=64)
-                if eng == "g":
-                    for off in range(9):
-                        u, v = divmod(off, 3)
-                        nc.gpsimd.tensor_tensor(
-                            out=pgall[:, off, :, :].rearrange("p (i j) t -> p i j t", i=nr),
-                            in0=XP[n][:, r0 + u:r0 + u + nr, v:v + 32, :],
-                            in1=NV[n][:, r0:r0 + nr, :].unsqueeze(3).to_broadcast([P, nr, 32, 4]),
-                            op=ALU.add)
-                else:
-                    ta = psum.tile([P, P], F32, name="ta", tag="tr", bufs=3)
-                    nc.tensor.transpose(ta[:], NV[n][:, r0:r0 + nr, :].rearrange("p i j -> p (i j)"),
-                                        ident[:])
-                    a2 = work.tile([P, P], F32, name="a2", tag="a2", bufs=2)
-                    nc.scalar.copy(out=a2[:], in_=ta[:])
-                    for off in range(9):
-                        u, v = divmod(off, 3)
-                        pp = psum.tile([P, 4, N], F32, name="pp", tag="tr", bufs=3)
+                        out=pg[:, k, 0:32 * rv, :].rearrange("p (i j) t -> p i j t", i=rv),
+                        in0=XP[n][:, r0 + u:r0 + u + rv, v:v + 32, :],
+                        in1=nvp[:].unsqueeze(3).to_broadcast([P, rv, 32, 4]), op=ALU.add)
+                    if rp:
+                        pp = psum.tile([P, 4, 32 * rp], F32, name="pp", tag="tr", bufs=3)
                         for t in range(4):
                             nc.tensor.matmul(out=pp[:, t, :], lhsT=a2[:], rhs=ident[:], is_transpose=True,
                                              start=(t == 0), stop=False)
-                        nc.tensor.matmul(out=pp[:].rearrange("p t (i j) -> p i j t", i=nr), lhsT=identb[:],
-                                         rhs=XP[n][:, r0 + u:r0 + u + nr, v:v + 32, :],
+                        nc.tensor.matmul(out=pp[:].rearrange("p t (i j) -> p i j t", i=rp), lhsT=identb[:],
+                                         rhs=XP[n][:, r0 + rv + u:r0 + nr + u, v:v + 32, :],
                                          start=False, stop=True)
-                        nc.scalar.copy(out=pgall[:, off, :, :], in_=pp[:].rearrange("p t x -> p x t"))
-                quant(pc, ps, 0, 8, pgall[:, 0:8, :, :])
-                quant(pc, ps, 8, 9, pgall[:, 8:9, :, :])
-            return pc, ps
+                        nc.scalar.copy(out=pg[:, k, 32 * rv:N, :], in_=pp[:].rearrange("p t x -> p x t"))
+                if prev is not None:
+                    finish(prev[0], prev[1])
+                prev = (pg, grp)
+            finish(prev[0], prev[1])
 
-        def block_b(n, r0, nr, last, pc, ps):
-            N = 32 * nr
-            per_bank = 512 // N
-            accs = []
-            for ot in range(4):
-                if ot % per_bank == 0:
-                    acc = psum.tile([P, per_bank, N], F32, name="acc", tag="acc", bufs=4)
-                a = acc[:, ot % per_bank, :]
-                accs.append(a)
-                for off in range(9):
-                    u, v = divmod(off, 3)
-                    ro = 3 * v + u
-                    nc.tensor.matmul_mx(
-                        out=a, lhsT=WC[:, ot, ro, :].bitcast(FP8X4), lhsT_scale=WS[:, ot, ro, :],
-                        rhs=pc[:, off, :].bitcast(FP8X4), rhs_scale=ps[:, off, :],
-                        start=(off == 0), stop=(off == 8))
-            res = work.tile([P, 4, N], F32, name="res", tag="res%d" % N, bufs=(2 if N == 256 else 3))
-            rel = work.tile([P, 4, N], F32, name="rel", tag="rel%d" % N, bufs=(2 if N == 256 else 3))
-            for ot in range(4):
-                nc.scalar.activation(out=res[:, ot, :], in_=accs[ot], func=ACT.Identity,
-                                     bias=b001[:, ot:ot + 1], scale=0.01)
-                nc.scalar.activation(out=rel[:, ot, :], in_=accs[ot], func=ACT.Relu,
-                                     bias=b099[:, ot:ot + 1], scale=0.99)
-            nvb = NV[n][:, r0:r0 + nr, :].rearrange("p i j -> p (i j)").unsqueeze(1).to_broadcast([P, 4, N])
-            if last == "g":
-                nc.gpsimd.tensor_tensor(out=res[:], in0=res[:], in1=nvb, op=ALU.subtract)
-                nc.gpsimd.tensor_tensor(out=res[:], in0=res[:], in1=rel[:], op=ALU.add)
-            else:
-                nc.vector.tensor_tensor(out=res[:], in0=res[:], in1=nvb, op=ALU.subtract)
-                nc.vector.tensor_tensor(out=res[:], in0=res[:], in1=rel[:], op=ALU.add)
             ov = out[n].rearrange("(a q h) i j -> h q a (i j)", a=4, q=64, h=2)
-            for h in range(2):
-                nc.sync.dma_start(out=ov[h][:, :, 32 * r0:32 * r0 + N], in_=res[64 * h:64 * h + 64, :, :])
+            nvf = NV[n][:, r0:r0 + nr, :].rearrange("p i j -> p (i j)")
+            for ot in range(4):
+                res = work.tile([P, N], F32, name="res", tag="res", bufs=4)
+                rel = work.tile([P, N], F32, name="rel", tag="rel", bufs=4)
+                nc.scalar.activation(out=res[:], in_=accs[ot][:], func=ACT.Identity,
+                                     bias=b001[:, ot:ot + 1], scale=0.01)
+                nc.scalar.activation(out=rel[:], in_=accs[ot][:], func=ACT.Relu,
+                                     bias=b099[:, ot:ot + 1], scale=0.99)
+                tt_on(add_eng, res[:], res[:], nvf, ALU.subtract)
+                tt_on(add_eng, res[:], res[:], rel[:], ALU.add)
+                for h in range(2):
+                    nc.sync.dma_start(out=ov[h][:, ot, 32 * r0:32 * r0 + N], in_=res[64 * h:64 * h + 64, :])
 
         stat_tiles(0)
-        pad_half(0, 0, "v")
-        sum_half(0, 0)
-        box_h(0, 0, "v")
-        box_v(0, 0, 15, "v")
-        sum_half(0, 1)
-        pad_half(0, 1, "s")
-        box_h(0, 1, "v")
-        box_v(0, 15, 32, "v")
-        pc0, ps0 = block_a(FIRST[0], FIRST[1], FIRST[2], FIRST[3])
-        wprep(0)
-        load_w(3)
-        wprep(1)
+        pad_rows(0, 0, SPLIT, "v")
+        sums(0, 0, SPLIT)
+        box_h(0, SPLIT, "v")
+        box_v(0, 0, SPLIT - 1, "v")
+        sums(0, SPLIT, 32)
+        pad_rows(0, SPLIT, 32, "s")
+        box_h(SPLIT, 32, "v")
+        box_v(0, SPLIT - 1, 32, "v")
+        for ot in range(4):
+            wprep(ot)
         stat_tiles(1)
-        for h in range(2):
-            sum_half(1, h)
-            box_h(1, h, "g")
+        sums(1, 0, 32)
+        box_h(0, 32, "g")
         box_v(1, 0, 32, "g")
-        wprep(2)
-        wprep(3)
-        for h in range(2):
-            pad_half(1, h, "s")
-        block_b(FIRST[0], FIRST[1], FIRST[2], FIRST[4], pc0, ps0)
+        pad_rows(1, 0, 16, "g")
+        pad_rows(1, 16, 32, "g")
         for blk in BLOCKS:
-            pcx, psx = block_a(blk[0], blk[1], blk[2], blk[3])
-            block_b(blk[0], blk[1], blk[2], blk[4], pcx, psx)
+            block(blk[0], blk[1], blk[2], blk[3], blk[4])

@@ -15,9 +15,12 @@ FLOPS = 2 * 512 * 4608 * 2048
 
 P = 128
 BLOCKS = [
-    (0, 0, 16, 4, "g"), (0, 16, 16, 4, "g"), (1, 0, 16, 4, "g"), (1, 16, 8, 4, "g"), (1, 24, 8, 0, "v"),
+    (0, 16, 4, "g", "g"), (0, 24, 4, "p", "g"), (0, 0, 8, "v", "g"), (0, 20, 4, "g", "g"),
+    (0, 28, 4, "p", "g"), (0, 8, 8, "v", "g"),
+    (1, 16, 4, "g", "g"), (1, 24, 4, "p", "g"), (1, 0, 8, "v", "g"), (1, 28, 4, "p", "g"),
+    (1, 8, 8, "v", "g"), (1, 20, 4, "v", "v"),
 ]
-WPRE = "sgsg"
+WPRE = "svsv"
 SPLIT = 17
 
 
@@ -42,12 +45,17 @@ def tile_conv2d_kernel(tc, xx, w, b, out):
             nc.sync.dma_start(out=xraw[0][0:64, :, cols], in_=xv0[0][:, :, cols])
             nc.scalar.dma_start(out=xraw[0][64:128, :, cols], in_=xv0[1][:, :, cols])
         wsb = []
-        for ot in range(4):
-            ws_t = wpool.tile([P, 4608], BF16, name="wsb%d" % ot, tag="wsb", bufs=4)
+
+        def load_w(ot):
+            ws_t = wpool.tile([P, 4608], BF16, name="wsb%d" % ot, tag="wsb", bufs=3)
             nc.sync.dma_start(out=ws_t[:], in_=wv[128 * ot:128 * ot + 128, :])
             wsb.append(ws_t)
+
+        load_w(0)
         nc.sync.dma_start(out=xraw[1][0:64, :, :], in_=xv1[0])
-        nc.sync.dma_start(out=xraw[1][64:128, :, :], in_=xv1[1])
+        nc.scalar.dma_start(out=xraw[1][64:128, :, :], in_=xv1[1])
+        load_w(1)
+        load_w(2)
         b_bf = const.tile([P, 4], BF16, name="b_bf")
         bv = b.rearrange("(a q h) -> h q a", a=4, q=64, h=2)
         with nc.allow_non_contiguous_dma(reason="512 bias values, one per partition and tile"):
@@ -179,81 +187,97 @@ def tile_conv2d_kernel(tc, xx, w, b, out):
                     in_=wg[:],
                 )
 
-        def block(n, r0, nr, rp, add_eng):
+        def quant(pc, ps, lo, hi, src):
+            nc.vector.quantize_mx(
+                out=pc[:, lo:hi, :].rearrange("p a x -> p (a x)").bitcast(FP8X4),
+                scales=ps[:, lo:hi, :].rearrange("p a x -> p (a x)"),
+                in_=src.rearrange("p a x t -> p (a x t)"))
+
+        def block_a(n, r0, nr, eng):
             N = 32 * nr
-            rv = nr - rp
-            pc = work.tile([P, 9, N], U32, name="pc", tag="pc", bufs=2, align_bytes=64)
-            ps = work.tile([P, 9, N], U8, name="ps", tag="ps", bufs=2, align_bytes=64)
-            nvp = psum.tile([P, rv, 32], F32, name="nvp", tag="nv", bufs=1)
-            nc.tensor.matmul(out=nvp[:].rearrange("p i j -> p (i j)"), lhsT=ident[:],
-                             rhs=NV[n][:, r0:r0 + rv, :].rearrange("p i j -> p (i j)"),
-                             start=True, stop=True)
-            a2 = None
-            if rp:
-                ta = psum.tile([P, P], F32, name="ta", tag="tr", bufs=3)
-                nc.tensor.transpose(ta[:], NV[n][:, r0 + rv:r0 + nr, :].rearrange("p i j -> p (i j)"),
-                                    ident[:])
-                a2 = work.tile([P, P], F32, name="a2", tag="a2", bufs=2)
-                nc.scalar.copy(out=a2[:], in_=ta[:])
-            accs = []
-            for ot in range(4):
-                acc = psum.tile([P, N], F32, name="acc%d" % ot, tag="acc", bufs=4)
-                accs.append(acc)
-
-            def finish(pg, grp):
-                lo, hi = grp[0], grp[-1] + 1
-                nc.vector.quantize_mx(
-                    out=pc[:, lo:hi, :].rearrange("p a x -> p (a x)").bitcast(FP8X4),
-                    scales=ps[:, lo:hi, :].rearrange("p a x -> p (a x)"),
-                    in_=pg[:, 0:hi - lo, :, :].rearrange("p a x t -> p (a x t)"))
-                for off in grp:
-                    u, v = divmod(off, 3)
-                    ro = 3 * v + u
-                    for ot in range(4):
-                        nc.tensor.matmul_mx(
-                            out=accs[ot][:], lhsT=WC[:, ot, ro, :].bitcast(FP8X4),
-                            lhsT_scale=WS[:, ot, ro, :],
-                            rhs=pc[:, off, :].bitcast(FP8X4), rhs_scale=ps[:, off, :],
-                            start=(off == 0), stop=(off == 8))
-
-            gsz = 1024 // N
-            prev = None
-            for g0 in range(0, 9, gsz):
-                grp = list(range(g0, min(g0 + gsz, 9)))
-                pg = work.tile([P, gsz, N, 4], BF16, name="pg", tag="pg", bufs=3, align_bytes=64)
-                for k, off in enumerate(grp):
+            nb = 2 if N == 256 else 4
+            pc = work.tile([P, 9, N], U32, name="pc", tag="pc%d" % N, bufs=nb, align_bytes=64)
+            ps = work.tile([P, 9, N], U8, name="ps", tag="ps%d" % N, bufs=nb, align_bytes=64)
+            if eng == "v":
+                nvp = psum.tile([P, nr, 32], F32, name="nvp", tag="nv", bufs=1)
+                nc.tensor.matmul(out=nvp[:].rearrange("p i j -> p (i j)"), lhsT=ident[:],
+                                 rhs=NV[n][:, r0:r0 + nr, :].rearrange("p i j -> p (i j)"),
+                                 start=True, stop=True)
+                pga = work.tile([P, 4, N, 4], BF16, name="pga", tag="pga", bufs=1, align_bytes=64)
+                pgb = work.tile([P, 4, N, 4], BF16, name="pgb", tag="pgb", bufs=1, align_bytes=64)
+                pgc = work.tile([P, 1, N, 4], BF16, name="pgc", tag="pgc", bufs=1, align_bytes=64)
+                dst = [pga, pgb, pgc]
+                for off in range(9):
                     u, v = divmod(off, 3)
                     nc.vector.tensor_tensor(
-                        out=pg[:, k, 0:32 * rv, :].rearrange("p (i j) t -> p i j t", i=rv),
-                        in0=XP[n][:, r0 + u:r0 + u + rv, v:v + 32, :],
-                        in1=nvp[:].unsqueeze(3).to_broadcast([P, rv, 32, 4]), op=ALU.add)
-                    if rp:
-                        pp = psum.tile([P, 4, 32 * rp], F32, name="pp", tag="tr", bufs=3)
+                        out=dst[off // 4][:, off % 4, :, :].rearrange("p (i j) t -> p i j t", i=nr),
+                        in0=XP[n][:, r0 + u:r0 + u + nr, v:v + 32, :],
+                        in1=nvp[:].unsqueeze(3).to_broadcast([P, nr, 32, 4]), op=ALU.add)
+                quant(pc, ps, 0, 4, pga[:])
+                quant(pc, ps, 4, 8, pgb[:])
+                quant(pc, ps, 8, 9, pgc[:])
+            else:
+                pgall = work.tile([P, 9, N, 4], BF16, name="pg" + eng, tag="pg" + eng,
+                                  bufs=1, align_bytes=64)
+                if eng == "g":
+                    for off in range(9):
+                        u, v = divmod(off, 3)
+                        nc.gpsimd.tensor_tensor(
+                            out=pgall[:, off, :, :].rearrange("p (i j) t -> p i j t", i=nr),
+                            in0=XP[n][:, r0 + u:r0 + u + nr, v:v + 32, :],
+                            in1=NV[n][:, r0:r0 + nr, :].unsqueeze(3).to_broadcast([P, nr, 32, 4]),
+                            op=ALU.add)
+                else:
+                    ta = psum.tile([P, P], F32, name="ta", tag="tr", bufs=3)
+                    nc.tensor.transpose(ta[:], NV[n][:, r0:r0 + nr, :].rearrange("p i j -> p (i j)"),
+                                        ident[:])
+                    a2 = work.tile([P, P], F32, name="a2", tag="a2", bufs=2)
+                    nc.scalar.copy(out=a2[:], in_=ta[:])
+                    for off in range(9):
+                        u, v = divmod(off, 3)
+                        pp = psum.tile([P, 4, N], F32, name="pp", tag="tr", bufs=3)
                         for t in range(4):
                             nc.tensor.matmul(out=pp[:, t, :], lhsT=a2[:], rhs=ident[:], is_transpose=True,
                                              start=(t == 0), stop=False)
-                        nc.tensor.matmul(out=pp[:].rearrange("p t (i j) -> p i j t", i=rp), lhsT=identb[:],
-                                         rhs=XP[n][:, r0 + rv + u:r0 + nr + u, v:v + 32, :],
+                        nc.tensor.matmul(out=pp[:].rearrange("p t (i j) -> p i j t", i=nr), lhsT=identb[:],
+                                         rhs=XP[n][:, r0 + u:r0 + u + nr, v:v + 32, :],
                                          start=False, stop=True)
-                        nc.scalar.copy(out=pg[:, k, 32 * rv:N, :], in_=pp[:].rearrange("p t x -> p x t"))
-                if prev is not None:
-                    finish(prev[0], prev[1])
-                prev = (pg, grp)
-            finish(prev[0], prev[1])
+                        nc.scalar.copy(out=pgall[:, off, :, :], in_=pp[:].rearrange("p t x -> p x t"))
+                quant(pc, ps, 0, 8, pgall[:, 0:8, :, :])
+                quant(pc, ps, 8, 9, pgall[:, 8:9, :, :])
+            return pc, ps
 
-            ov = out[n].rearrange("(a q h) i j -> h q a (i j)", a=4, q=64, h=2)
-            nvf = NV[n][:, r0:r0 + nr, :].rearrange("p i j -> p (i j)")
+        def block_b(n, r0, nr, last, pc, ps):
+            N = 32 * nr
+            per_bank = 512 // N
+            accs = []
             for ot in range(4):
-                res = work.tile([P, N], F32, name="res", tag="res", bufs=4)
-                rel = work.tile([P, N], F32, name="rel", tag="rel", bufs=4)
-                nc.scalar.activation(out=res[:], in_=accs[ot][:], func=ACT.Identity,
+                if ot % per_bank == 0:
+                    acc = psum.tile([P, per_bank, N], F32, name="acc", tag="acc", bufs=4)
+                a = acc[:, ot % per_bank, :]
+                accs.append(a)
+                for off in range(9):
+                    u, v = divmod(off, 3)
+                    ro = 3 * v + u
+                    nc.tensor.matmul_mx(
+                        out=a, lhsT=WC[:, ot, ro, :].bitcast(FP8X4), lhsT_scale=WS[:, ot, ro, :],
+                        rhs=pc[:, off, :].bitcast(FP8X4), rhs_scale=ps[:, off, :],
+                        start=(off == 0), stop=(off == 8))
+            res = work.tile([P, 4, N], F32, name="res", tag="res%d" % N, bufs=3)
+            for ot in range(4):
+                nc.scalar.activation(out=res[:, ot, :], in_=accs[ot], func=ACT.Identity,
                                      bias=b001[:, ot:ot + 1], scale=0.01)
-                nc.scalar.activation(out=rel[:], in_=accs[ot][:], func=ACT.Relu,
-                                     bias=b099[:, ot:ot + 1], scale=0.99)
-                tt_on(add_eng, res[:], res[:], nvf, ALU.subtract)
-                tt_on(add_eng, res[:], res[:], rel[:], ALU.add)
-                for h in range(2):
-                    nc.sync.dma_start(out=ov[h][:, ot, 32 * r0:32 * r0 + N], in_=res[64 * h:64 * h + 64, :])
+            for ot in range(4):
+                nc.vector.scalar_tensor_tensor(out=res[:, ot, :], in0=accs[ot], scalar=b32[:, ot:ot + 1],
+                                               in1=res[:, ot, :], op0=ALU.add, op1=ALU.max)
+            nvb = NV[n][:, r0:r0 + nr, :].rearrange("p i j -> p (i j)").unsqueeze(1).to_broadcast([P, 4, N])
+            if last == "g":
+                nc.gpsimd.tensor_tensor(out=res[:], in0=res[:], in1=nvb, op=ALU.subtract)
+            else:
+                nc.vector.tensor_tensor(out=res[:], in0=res[:], in1=nvb, op=ALU.subtract)
+            ov = out[n].rearrange("(a q h) i j -> h q a (i j)", a=4, q=64, h=2)
+            for h in range(2):
+                nc.sync.dma_start(out=ov[h][:, :, 32 * r0:32 * r0 + N], in_=res[64 * h:64 * h + 64, :, :])
 
         stat_tiles(0)
         pad_rows(0, 0, SPLIT, "v")
@@ -264,13 +288,16 @@ def tile_conv2d_kernel(tc, xx, w, b, out):
         pad_rows(0, SPLIT, 32, "s")
         box_h(SPLIT, 32, "v")
         box_v(0, SPLIT - 1, 32, "v")
-        for ot in range(4):
-            wprep(ot)
+        wprep(0)
+        load_w(3)
         stat_tiles(1)
         sums(1, 0, 32)
         box_h(0, 32, "g")
         box_v(1, 0, 32, "g")
-        pad_rows(1, 0, 16, "g")
-        pad_rows(1, 16, 32, "g")
+        pad_rows(1, 0, 32, "v")
+        wprep(1)
+        wprep(2)
+        wprep(3)
         for blk in BLOCKS:
-            block(blk[0], blk[1], blk[2], blk[3], blk[4])
+            pcx, psx = block_a(blk[0], blk[1], blk[2], blk[3])
+            block_b(blk[0], blk[1], blk[2], blk[4], pcx, psx)

@@ -263,18 +263,20 @@ def tile_conv2d_kernel(tc, xx, w, b, out):
                         out=a, lhsT=WC[:, ot, ro, :].bitcast(FP8X4), lhsT_scale=WS[:, ot, ro, :],
                         rhs=pc[:, off, :].bitcast(FP8X4), rhs_scale=ps[:, off, :],
                         start=(off == 0), stop=(off == 8))
-            res = work.tile([P, 4, N], F32, name="res", tag="res%d" % N, bufs=3)
+            res = work.tile([P, 4, N], F32, name="res", tag="res%d" % N, bufs=2)
+            rel = work.tile([P, 4, N], F32, name="rel", tag="rel%d" % N, bufs=2)
             for ot in range(4):
                 nc.scalar.activation(out=res[:, ot, :], in_=accs[ot], func=ACT.Identity,
                                      bias=b001[:, ot:ot + 1], scale=0.01)
-            for ot in range(4):
-                nc.vector.scalar_tensor_tensor(out=res[:, ot, :], in0=accs[ot], scalar=b32[:, ot:ot + 1],
-                                               in1=res[:, ot, :], op0=ALU.add, op1=ALU.max)
+                nc.scalar.activation(out=rel[:, ot, :], in_=accs[ot], func=ACT.Relu,
+                                     bias=b099[:, ot:ot + 1], scale=0.99)
             nvb = NV[n][:, r0:r0 + nr, :].rearrange("p i j -> p (i j)").unsqueeze(1).to_broadcast([P, 4, N])
             if last == "g":
                 nc.gpsimd.tensor_tensor(out=res[:], in0=res[:], in1=nvb, op=ALU.subtract)
+                nc.gpsimd.tensor_tensor(out=res[:], in0=res[:], in1=rel[:], op=ALU.add)
             else:
                 nc.vector.tensor_tensor(out=res[:], in0=res[:], in1=nvb, op=ALU.subtract)
+                nc.vector.tensor_tensor(out=res[:], in0=res[:], in1=rel[:], op=ALU.add)
             ov = out[n].rearrange("(a q h) i j -> h q a (i j)", a=4, q=64, h=2)
             for h in range(2):
                 nc.sync.dma_start(out=ov[h][:, :, 32 * r0:32 * r0 + N], in_=res[64 * h:64 * h + 64, :, :])

@@ -15,10 +15,10 @@ FLOPS = 2 * 512 * 4608 * 2048
 
 P = 128
 BLOCKS = [
-    (0, 16, 4, "g", "g"), (0, 24, 4, "p", "g"), (0, 0, 8, "v", "g"), (0, 20, 4, "g", "g"),
-    (0, 28, 4, "p", "g"), (0, 8, 8, "v", "g"),
-    (1, 16, 4, "g", "g"), (1, 24, 4, "p", "g"), (1, 0, 8, "v", "g"), (1, 28, 4, "p", "g"),
-    (1, 8, 8, "v", "g"), (1, 20, 4, "v", "v"),
+    (0, 24, 4, "p", "v"), (0, 0, 8, "v", "v"), (0, 28, 4, "p", "v"), (0, 8, 8, "v", "v"),
+    (0, 16, 8, "v", "v"),
+    (1, 24, 4, "p", "v"), (1, 0, 8, "v", "v"), (1, 28, 4, "p", "v"), (1, 8, 8, "v", "v"),
+    (1, 16, 4, "v", "v"), (1, 20, 4, "v", "v"),
 ]
 WPRE = "svsv"
 SPLIT = 17
@@ -263,20 +263,18 @@ def tile_conv2d_kernel(tc, xx, w, b, out):
                         out=a, lhsT=WC[:, ot, ro, :].bitcast(FP8X4), lhsT_scale=WS[:, ot, ro, :],
                         rhs=pc[:, off, :].bitcast(FP8X4), rhs_scale=ps[:, off, :],
                         start=(off == 0), stop=(off == 8))
-            res = work.tile([P, 4, N], F32, name="res", tag="res%d" % N, bufs=2)
-            rel = work.tile([P, 4, N], F32, name="rel", tag="rel%d" % N, bufs=2)
+            res = work.tile([P, 4, N], F32, name="res", tag="res%d" % N, bufs=3)
             for ot in range(4):
                 nc.scalar.activation(out=res[:, ot, :], in_=accs[ot], func=ACT.Identity,
                                      bias=b001[:, ot:ot + 1], scale=0.01)
-                nc.scalar.activation(out=rel[:, ot, :], in_=accs[ot], func=ACT.Relu,
-                                     bias=b099[:, ot:ot + 1], scale=0.99)
+            for ot in range(4):
+                nc.vector.scalar_tensor_tensor(out=res[:, ot, :], in0=accs[ot], scalar=b32[:, ot:ot + 1],
+                                               in1=res[:, ot, :], op0=ALU.add, op1=ALU.max)
             nvb = NV[n][:, r0:r0 + nr, :].rearrange("p i j -> p (i j)").unsqueeze(1).to_broadcast([P, 4, N])
             if last == "g":
                 nc.gpsimd.tensor_tensor(out=res[:], in0=res[:], in1=nvb, op=ALU.subtract)
-                nc.gpsimd.tensor_tensor(out=res[:], in0=res[:], in1=rel[:], op=ALU.add)
             else:
                 nc.vector.tensor_tensor(out=res[:], in0=res[:], in1=nvb, op=ALU.subtract)
-                nc.vector.tensor_tensor(out=res[:], in0=res[:], in1=rel[:], op=ALU.add)
             ov = out[n].rearrange("(a q h) i j -> h q a (i j)", a=4, q=64, h=2)
             for h in range(2):
                 nc.sync.dma_start(out=ov[h][:, :, 32 * r0:32 * r0 + N], in_=res[64 * h:64 * h + 64, :, :])

@@ -15,9 +15,9 @@ FLOPS = 2 * 512 * 4608 * 2048
 
 P = 128
 BLOCKS = [
-    (0, 24, 4, "p", "v"), (0, 0, 8, "v", "v"), (0, 28, 4, "p", "v"), (0, 8, 8, "v", "v"),
-    (0, 16, 8, "v", "v"),
-    (1, 24, 4, "p", "v"), (1, 0, 8, "v", "v"), (1, 28, 4, "p", "v"), (1, 8, 8, "v", "v"),
+    (0, 24, 4, "p", "g"), (0, 0, 8, "v", "g"), (0, 28, 4, "p", "g"), (0, 8, 8, "v", "g"),
+    (0, 16, 8, "v", "g"),
+    (1, 24, 4, "p", "g"), (1, 0, 8, "v", "g"), (1, 28, 4, "p", "g"), (1, 8, 8, "v", "g"),
     (1, 16, 4, "v", "v"), (1, 20, 4, "v", "v"),
 ]
 WPRE = "svsv"
@@ -263,18 +263,20 @@ def tile_conv2d_kernel(tc, xx, w, b, out):
                         out=a, lhsT=WC[:, ot, ro, :].bitcast(FP8X4), lhsT_scale=WS[:, ot, ro, :],
                         rhs=pc[:, off, :].bitcast(FP8X4), rhs_scale=ps[:, off, :],
                         start=(off == 0), stop=(off == 8))
-            res = work.tile([P, 4, N], F32, name="res", tag="res%d" % N, bufs=3)
+            res = work.tile([P, 4, N], F32, name="res", tag="res%d" % N, bufs=2)
+            rel = work.tile([P, 4, N], F32, name="rel", tag="rel%d" % N, bufs=2)
             for ot in range(4):
                 nc.scalar.activation(out=res[:, ot, :], in_=accs[ot], func=ACT.Identity,
                                      bias=b001[:, ot:ot + 1], scale=0.01)
-            for ot in range(4):
-                nc.vector.scalar_tensor_tensor(out=res[:, ot, :], in0=accs[ot], scalar=b32[:, ot:ot + 1],
-                                               in1=res[:, ot, :], op0=ALU.add, op1=ALU.max)
+                nc.scalar.activation(out=rel[:, ot, :], in_=accs[ot], func=ACT.Relu,
+                                     bias=b099[:, ot:ot + 1], scale=0.99)
             nvb = NV[n][:, r0:r0 + nr, :].rearrange("p i j -> p (i j)").unsqueeze(1).to_broadcast([P, 4, N])
             if last == "g":
                 nc.gpsimd.tensor_tensor(out=res[:], in0=res[:], in1=nvb, op=ALU.subtract)
+                nc.gpsimd.tensor_tensor(out=res[:], in0=res[:], in1=rel[:], op=ALU.add)
             else:
                 nc.vector.tensor_tensor(out=res[:], in0=res[:], in1=nvb, op=ALU.subtract)
+                nc.vector.tensor_tensor(out=res[:], in0=res[:], in1=rel[:], op=ALU.add)
             ov = out[n].rearrange("(a q h) i j -> h q a (i j)", a=4, q=64, h=2)
             for h in range(2):
                 nc.sync.dma_start(out=ov[h][:, :, 32 * r0:32 * r0 + N], in_=res[64 * h:64 * h + 64, :, :])

from contextlib import ExitStack

import concourse.mybir as mybir
from concourse.masks import make_identity

F32 = mybir.dt.float32
BF16 = mybir.dt.bfloat16
U32 = mybir.dt.uint32
U8 = mybir.dt.uint8
FP8X4 = mybir.dt.float8_e4m3fn_x4
ALU = mybir.AluOpType
ACT = mybir.ActivationFunctionType

FLOPS = 2 * 512 * 4608 * 2048

P = 128
BLOCKS = [
    (0, 24, 4, "p", "g"), (0, 0, 8, "v", "g"), (0, 28, 4, "p", "g"), (0, 8, 8, "v", "g"),
    (0, 16, 8, "v", "g"),
    (1, 24, 4, "p", "g"), (1, 0, 8, "v", "g"), (1, 28, 4, "p", "g"), (1, 8, 8, "v", "g"),
    (1, 16, 4, "v", "v"), (1, 20, 4, "v", "v"),
]
WPRE = "svsv"
SPLIT = 17


def tile_conv2d_kernel(tc, xx, w, b, out):
    nc = tc.nc
    with ExitStack() as ctx:
        const = ctx.enter_context(tc.tile_pool(name="const", bufs=1))
        xpool = ctx.enter_context(tc.tile_pool(name="xpool", bufs=2))
        wpool = ctx.enter_context(tc.tile_pool(name="wpool", bufs=2))
        stat = ctx.enter_context(tc.tile_pool(name="stat", bufs=1))
        work = ctx.enter_context(tc.tile_pool(name="work", bufs=2))
        psum = ctx.enter_context(tc.psum_pool(name="psum", bufs=1))

        xraw = []
        for n in range(2):
            xr = xpool.tile([P, 4, 1024], BF16, name="xraw%d" % n, tag="xraw", bufs=2)
            xraw.append(xr)
        xv0 = xx[0].rearrange("(t q m) h w -> m q t (h w)", t=4, q=64, m=2)
        xv1 = xx[1].rearrange("(t q m) h w -> m q t (h w)", t=4, q=64, m=2)
        wv = w.rearrange("o c a b -> o (c a b)")
        for cols in (slice(0, 32 * SPLIT), slice(32 * SPLIT, 1024)):
            nc.sync.dma_start(out=xraw[0][0:64, :, cols], in_=xv0[0][:, :, cols])
            nc.scalar.dma_start(out=xraw[0][64:128, :, cols], in_=xv0[1][:, :, cols])
        wsb = []

        def load_w(ot):
            ws_t = wpool.tile([P, 4608], BF16, name="wsb%d" % ot, tag="wsb", bufs=3)
            nc.sync.dma_start(out=ws_t[:], in_=wv[128 * ot:128 * ot + 128, :])
            wsb.append(ws_t)

        load_w(0)
        nc.sync.dma_start(out=xraw[1][0:64, :, :], in_=xv1[0])
        nc.scalar.dma_start(out=xraw[1][64:128, :, :], in_=xv1[1])
        load_w(1)
        load_w(2)
        b_bf = const.tile([P, 4], BF16, name="b_bf")
        bv = b.rearrange("(a q h) -> h q a", a=4, q=64, h=2)
        with nc.allow_non_contiguous_dma(reason="512 bias values, one per partition and tile"):
            nc.scalar.dma_start(out=b_bf[0:64, :], in_=bv[0])
            nc.scalar.dma_start(out=b_bf[64:128, :], in_=bv[1])

        sel = const.tile([P, P], BF16, name="sel")
        nc.vector.memset(sel[:], 0.0)
        nc.vector.memset(sel[0:64, 0:64], 1.0)
        nc.vector.memset(sel[64:128, 64:128], 1.0)
        warm = const.tile([P, 8], F32, name="warm")
        nc.scalar.activation(out=warm[:], in_=sel[:, 0:8], func=ACT.Relu)
        ident = const.tile([P, P], F32, name="ident")
        make_identity(nc, ident[:])
        identb = const.tile([P, P], BF16, name="identb")
        nc.vector.tensor_copy(out=identb[:], in_=ident[:])
        perm = const.tile([P, P], F32, name="perm")
        nc.vector.tensor_copy(
            out=perm[:].rearrange("p (h q) -> p h q", h=2),
            in_=ident[:].rearrange("p (q h) -> p h q", h=2),
        )
        b32 = const.tile([P, 4], F32, name="b32")
        nc.vector.tensor_copy(out=b32[:], in_=b_bf[:])
        b001 = const.tile([P, 4], F32, name="b001")
        nc.vector.tensor_scalar_mul(out=b001[:], in0=b32[:], scalar1=0.01)
        b099 = const.tile([P, 4], F32, name="b099")
        nc.vector.tensor_scalar_mul(out=b099[:], in0=b32[:], scalar1=0.99)

        WC = const.tile([P, 4, 9, P], U32, name="WC", align_bytes=64)
        WS = const.tile([P, 4, 9, P], U8, name="WS", align_bytes=64)

        XP = []
        NV = []
        for n in range(2):
            xp_t = const.tile([P, 34, 36, 4], BF16, name="XP%d" % n)
            XP.append(xp_t)
            nv_t = const.tile([P, 32, 32], F32, name="NV%d" % n)
            NV.append(nv_t)

        def copy_on(eng, out_ap, in_ap):
            if eng == "v":
                nc.vector.tensor_copy(out=out_ap, in_=in_ap)
            elif eng == "g":
                nc.gpsimd.tensor_scalar(out=out_ap, in0=in_ap, scalar1=1.0, scalar2=0.0,
                                        op0=ALU.mult, op1=ALU.add)
            else:
                nc.scalar.copy(out=out_ap, in_=in_ap)

        def tt_on(eng, out_ap, a_ap, b_ap, op):
            if eng == "v":
                nc.vector.tensor_tensor(out=out_ap, in0=a_ap, in1=b_ap, op=op)
            else:
                nc.gpsimd.tensor_tensor(out=out_ap, in0=a_ap, in1=b_ap, op=op)

        def pad_rows(n, ra, rb, eng):
            xp = XP[n]
            rows = slice(1 + ra, 1 + rb)
            copy_on(eng, xp[:, rows, 1:33, :],
                    xraw[n][:, :, 32 * ra:32 * rb].rearrange("p t (i j) -> p i j t", i=rb - ra))
            copy_on(eng, xp[:, rows, 0:1, :], xp[:, rows, 1:2, :])
            copy_on(eng, xp[:, rows, 33:34, :], xp[:, rows, 32:33, :])
            if ra == 0:
                copy_on(eng, xp[:, 0:1, 0:34, :], xp[:, 1:2, 0:34, :])
            if rb == 32:
                copy_on(eng, xp[:, 33:34, 0:34, :], xp[:, 32:33, 0:34, :])

        st = {}

        def stat_tiles(n):
            st["sp"] = stat.tile([P, 32, 34], F32, name="sp%d" % n, tag="sp")
            st["tm"] = stat.tile([P, 32, 32], F32, name="tm%d" % n, tag="tm")
            st["hp"] = stat.tile([P, 34, 32], F32, name="hp%d" % n, tag="hp")

        def sums(n, ra, rb):
            sp = st["sp"]
            for r in range(ra, rb, 16):
                re = min(r + 16, rb)
                ssum = psum.tile([P, re - r, 32], F32, name="ssum", tag="tr", bufs=3)
                for t in range(4):
                    nc.tensor.matmul(out=ssum[:].rearrange("p i j -> p (i j)"), lhsT=sel[:],
                                     rhs=xraw[n][:, t, 32 * r:32 * re],
                                     start=(t == 0), stop=(t == 3))
                nc.scalar.activation(out=sp[:, r:re, 1:33], in_=ssum[:], func=ACT.Copy,
                                     scale=-1.0 / 2304.0)
                nc.scalar.activation(out=sp[:, r:re, 0:1], in_=ssum[:, :, 0:1], func=ACT.Copy,
                                     scale=-1.0 / 2304.0)
                nc.scalar.activation(out=sp[:, r:re, 33:34], in_=ssum[:, :, 31:32], func=ACT.Copy,
                                     scale=-1.0 / 2304.0)

        def box_h(ra, rb, eng):
            sp, tm, hp = st["sp"], st["tm"], st["hp"]
            tt_on(eng, tm[:, ra:rb, :], sp[:, ra:rb, 0:32], sp[:, ra:rb, 1:33], ALU.add)
            tt_on(eng, hp[:, 1 + ra:1 + rb, :], tm[:, ra:rb, :], sp[:, ra:rb, 2:34], ALU.add)
            if ra == 0:
                copy_on(eng, hp[:, 0:1, :], hp[:, 1:2, :])
            if rb == 32:
                copy_on(eng, hp[:, 33:34, :], hp[:, 32:33, :])

        def box_v(n, lo, hi, eng):
            hp, tm = st["hp"], st["tm"]
            tt_on(eng, tm[:, lo:hi, :], hp[:, lo:hi, :], hp[:, lo + 1:hi + 1, :], ALU.add)
            tt_on(eng, NV[n][:, lo:hi, :], tm[:, lo:hi, :], hp[:, lo + 2:hi + 2, :], ALU.add)

        def wprep(ot):
            eng = WPRE[ot]
            wview = wsb[ot][:].rearrange("o (u e q m r) -> o r u m q e", u=2, e=2, q=64, m=2, r=9)
            for g0, R in ((0, 4), (4, 4), (8, 1)):
                wr = wpool.tile([P, R, 2, 2, 64, 2], BF16, name="wr", tag="wr", bufs=2)
                for k in range(R):
                    if eng == "v":
                        nc.vector.tensor_copy(out=wr[:, k, :, :, :, :], in_=wview[:, g0 + k, :, :, :, :])
                    else:
                        for u in range(2):
                            copy_on(eng, wr[:, k, u, :, :, :], wview[:, g0 + k, u, :, :, :])
                wg = wpool.tile([P, R * 512], BF16, name="wg", tag="wg", bufs=2, align_bytes=64)
                wrf = wr[:].rearrange("o r u m q e -> o (r u m q e)").bitcast(F32).rearrange(
                    "o (r u p) -> o r u p", r=R, u=2)
                wgf = wg[:].bitcast(F32).rearrange("p (r o u) -> p r o u", r=R, u=2)
                for k0 in range(0, R, 2):
                    RR = min(2, R - k0)
                    tp = psum.tile([P, 2, RR, P], F32, name="tp", tag="tr", bufs=3)
                    for rr in range(RR):
                        for u in range(2):
                            nc.tensor.transpose(tp[:, u, rr, :], wrf[:, k0 + rr, u, :], perm[:])
                    nc.scalar.copy(out=wgf[:, k0:k0 + RR, :, :], in_=tp[:].rearrange("p u r o -> p r o u"))
                nc.vector.quantize_mx(
                    out=WC[:, ot, g0:g0 + R, :].rearrange("p r o -> p (r o)").bitcast(FP8X4),
                    scales=WS[:, ot, g0:g0 + R, :].rearrange("p r o -> p (r o)"),
                    in_=wg[:],
                )

        def quant(pc, ps, lo, hi, src):
            nc.vector.quantize_mx(
                out=pc[:, lo:hi, :].rearrange("p a x -> p (a x)").bitcast(FP8X4),
                scales=ps[:, lo:hi, :].rearrange("p a x -> p (a x)"),
                in_=src.rearrange("p a x t -> p (a x t)"))

        def block_a(n, r0, nr, eng):
            N = 32 * nr
            nb = 2 if N == 256 else 4
            pc = work.tile([P, 9, N], U32, name="pc", tag="pc%d" % N, bufs=nb, align_bytes=64)
            ps = work.tile([P, 9, N], U8, name="ps", tag="ps%d" % N, bufs=nb, align_bytes=64)
            if eng == "v":
                nvp = psum.tile([P, nr, 32], F32, name="nvp", tag="nv", bufs=1)
                nc.tensor.matmul(out=nvp[:].rearrange("p i j -> p (i j)"), lhsT=ident[:],
                                 rhs=NV[n][:, r0:r0 + nr, :].rearrange("p i j -> p (i j)"),
                                 start=True, stop=True)
                pga = work.tile([P, 4, N, 4], BF16, name="pga", tag="pga", bufs=1, align_bytes=64)
                pgb = work.tile([P, 4, N, 4], BF16, name="pgb", tag="pgb", bufs=1, align_bytes=64)
                pgc = work.tile([P, 1, N, 4], BF16, name="pgc", tag="pgc", bufs=1, align_bytes=64)
                dst = [pga, pgb, pgc]
                for off in range(9):
                    u, v = divmod(off, 3)
                    nc.vector.tensor_tensor(
                        out=dst[off // 4][:, off % 4, :, :].rearrange("p (i j) t -> p i j t", i=nr),
                        in0=XP[n][:, r0 + u:r0 + u + nr, v:v + 32, :],
                        in1=nvp[:].unsqueeze(3).to_broadcast([P, nr, 32, 4]), op=ALU.add)
                quant(pc, ps, 0, 4, pga[:])
                quant(pc, ps, 4, 8, pgb[:])
                quant(pc, ps, 8, 9, pgc[:])
            else:
                pgall = work.tile([P, 9, N, 4], BF16, name="pg" + eng, tag="pg" + eng,
                                  bufs=1, align_bytes=64)
                if eng == "g":
                    for off in range(9):
                        u, v = divmod(off, 3)
                        nc.gpsimd.tensor_tensor(
                            out=pgall[:, off, :, :].rearrange("p (i j) t -> p i j t", i=nr),
                            in0=XP[n][:, r0 + u:r0 + u + nr, v:v + 32, :],
                            in1=NV[n][:, r0:r0 + nr, :].unsqueeze(3).to_broadcast([P, nr, 32, 4]),
                            op=ALU.add)
                else:
                    ta = psum.tile([P, P], F32, name="ta", tag="tr", bufs=3)
                    nc.tensor.transpose(ta[:], NV[n][:, r0:r0 + nr, :].rearrange("p i j -> p (i j)"),
                                        ident[:])
                    a2 = work.tile([P, P], F32, name="a2", tag="a2", bufs=2)
                    nc.scalar.copy(out=a2[:], in_=ta[:])
                    for off in range(9):
                        u, v = divmod(off, 3)
                        pp = psum.tile([P, 4, N], F32, name="pp", tag="tr", bufs=3)
                        for t in range(4):
                            nc.tensor.matmul(out=pp[:, t, :], lhsT=a2[:], rhs=ident[:], is_transpose=True,
                                             start=(t == 0), stop=False)
                        nc.tensor.matmul(out=pp[:].rearrange("p t (i j) -> p i j t", i=nr), lhsT=identb[:],
                                         rhs=XP[n][:, r0 + u:r0 + u + nr, v:v + 32, :],
                                         start=False, stop=True)
                        nc.scalar.copy(out=pgall[:, off, :, :], in_=pp[:].rearrange("p t x -> p x t"))
                quant(pc, ps, 0, 8, pgall[:, 0:8, :, :])
                quant(pc, ps, 8, 9, pgall[:, 8:9, :, :])
            return pc, ps

        def block_b(n, r0, nr, last, pc, ps):
            N = 32 * nr
            per_bank = 512 // N
            accs = []
            for ot in range(4):
                if ot % per_bank == 0:
                    acc = psum.tile([P, per_bank, N], F32, name="acc", tag="acc", bufs=4)
                a = acc[:, ot % per_bank, :]
                accs.append(a)
                for off in range(9):
                    u, v = divmod(off, 3)
                    ro = 3 * v + u
                    nc.tensor.matmul_mx(
                        out=a, lhsT=WC[:, ot, ro, :].bitcast(FP8X4), lhsT_scale=WS[:, ot, ro, :],
                        rhs=pc[:, off, :].bitcast(FP8X4), rhs_scale=ps[:, off, :],
                        start=(off == 0), stop=(off == 8))
            res = work.tile([P, 4, N], F32, name="res", tag="res%d" % N, bufs=2)
            rel = work.tile([P, 4, N], F32, name="rel", tag="rel%d" % N, bufs=2)
            for ot in range(4):
                nc.scalar.activation(out=res[:, ot, :], in_=accs[ot], func=ACT.Identity,
                                     bias=b001[:, ot:ot + 1], scale=0.01)
                nc.scalar.activation(out=rel[:, ot, :], in_=accs[ot], func=ACT.Relu,
                                     bias=b099[:, ot:ot + 1], scale=0.99)
            nvb = NV[n][:, r0:r0 + nr, :].rearrange("p i j -> p (i j)").unsqueeze(1).to_broadcast([P, 4, N])
            if last == "g":
                nc.gpsimd.tensor_tensor(out=res[:], in0=res[:], in1=nvb, op=ALU.subtract)
                nc.gpsimd.tensor_tensor(out=res[:], in0=res[:], in1=rel[:], op=ALU.add)
            else:
                nc.vector.tensor_tensor(out=res[:], in0=res[:], in1=nvb, op=ALU.subtract)
                nc.vector.tensor_tensor(out=res[:], in0=res[:], in1=rel[:], op=ALU.add)
            ov = out[n].rearrange("(a q h) i j -> h q a (i j)", a=4, q=64, h=2)
            for h in range(2):
                nc.sync.dma_start(out=ov[h][:, :, 32 * r0:32 * r0 + N], in_=res[64 * h:64 * h + 64, :, :])

        stat_tiles(0)
        pad_rows(0, 0, SPLIT, "v")
        sums(0, 0, SPLIT)
        box_h(0, SPLIT, "v")
        box_v(0, 0, SPLIT - 1, "v")
        sums(0, SPLIT, 32)
        pad_rows(0, SPLIT, 32, "s")
        box_h(SPLIT, 32, "v")
        box_v(0, SPLIT - 1, 32, "v")
        wprep(0)
        load_w(3)
        stat_tiles(1)
        sums(1, 0, 32)
        box_h(0, 32, "g")
        box_v(1, 0, 32, "g")
        pad_rows(1, 0, 32, "v")
        wprep(1)
        wprep(2)
        wprep(3)
        for blk in BLOCKS:
            pcx, psx = block_a(blk[0], blk[1], blk[2], blk[3])
            block_b(blk[0], blk[1], blk[2], blk[4], pcx, psx)
